import numpy as np
import ml_dtypes


def mxq(x, axis, fmt="e4m3"):
    dtype, down = {"e4m3": (ml_dtypes.float8_e4m3fn, 7), "e5m2": (ml_dtypes.float8_e5m2, 14)}[fmt]
    v = np.moveaxis(np.asarray(x, np.float32).astype(ml_dtypes.bfloat16).astype(np.float64), axis, -1)
    blocks = v.reshape(v.shape[:-1] + (-1, 32))
    amax = np.abs(blocks).max(-1, keepdims=True)
    byte = np.maximum(np.where(amax > 0, np.frexp(amax)[1] - 1 + 127, 0) - down, 1)
    scale = np.exp2(byte - 127.0)
    codes = (blocks / scale).astype(np.float32).astype(dtype).astype(np.float64)
    return np.moveaxis((codes * scale).reshape(v.shape), -1, axis)


WIDE = False


def mx_kscale(k):
    if not WIDE:
        return np.ones(k)
    levels = np.array([10, -10, 5, -5, 0])
    a = np.random.permutation(np.resize(levels, k // 512 * 4)).reshape(k // 512, 4)
    idx = np.arange(k)
    return np.exp2(a[idx // 512, idx % 128 // 32])


BF16 = ml_dtypes.bfloat16


def bf(x):
    return np.asarray(x, np.float32).astype(BF16)


def f64(x):
    return np.asarray(x).astype(np.float64)


B, D, U, L, G, P, NG = 512, 1024, 256, 3, 5, 3, 4
NB = G + P
C = (1 + L) * U


def silu(v):
    return v / (1.0 + np.exp(-v))


def knots():
    return -1.0 + (2.0 / G) * np.arange(-P, G + P + 1)


def bspline_basis(x, grid, k):
    xe = x[..., None]
    b = np.where((xe >= grid[:-1]) & (xe < grid[1:]), 1.0, 0.0)
    for p in range(1, k + 1):
        left = (xe - grid[:-(p + 1)]) / (grid[p:-1] - grid[:-(p + 1)]) * b[..., :-1]
        right = (grid[p + 1:] - xe) / (grid[p + 1:] - grid[1:-p]) * b[..., 1:]
        b = left + right
    return b


def setup_inputs():
    t = mx_kscale(C)
    tk = t[U:].reshape(L, 1, U)
    return {
        "x": bf(np.random.standard_normal((B, D))),
        "lstm_out": bf(np.random.standard_normal((B, U)) * 0.3 * t[:U]),
        "kan_base_w": bf(np.random.standard_normal((L, D, U)) / np.sqrt(D) * tk),
        "kan_spline_w": bf(np.random.standard_normal((L, D * NB, U)) / np.sqrt(D) * tk),
        "combine_w": bf(np.random.standard_normal((C, U)) / np.sqrt(C) / t[:, None]),
        "combine_b": bf(np.random.standard_normal(U) * 0.2),
    }


def reference(x, lstm_out, kan_base_w, kan_spline_w, combine_w, combine_b):
    x = f64(x)
    bases = bspline_basis(x, knots(), P)
    base_out = mxq(silu(x), 1, "e4m3") @ mxq(f64(kan_base_w), 1, "e4m3")
    spline_out = mxq(bases.reshape(B, D * NB), 1, "e4m3") @ mxq(f64(kan_spline_w), 1, "e4m3")
    kan_out = base_out + spline_out
    kan_concat = kan_out.transpose(1, 0, 2).reshape(B, L * U)
    combined = np.concatenate([f64(lstm_out), kan_concat], axis=-1)
    return (mxq(combined, 1, "e4m3") @ mxq(f64(combine_w), 0, "e4m3")) + f64(combine_b)

@@ -1,0 +1,229 @@
+import math
+from contextlib import ExitStack
+
+import concourse.mybir as mybir
+from concourse.masks import make_identity
+
+BF16 = mybir.dt.bfloat16
+F32 = mybir.dt.float32
+U32 = mybir.dt.uint32
+U8 = mybir.dt.uint8
+FP8X4 = mybir.dt.float8_e4m3fn_x4
+ACT = mybir.ActivationFunctionType
+ALU = mybir.AluOpType
+
+P = 128
+PACK = 4
+K_PASS = P * PACK
+
+B, D, U, L, NB = 512, 1024, 256, 3, 8
+FOLD = NB // 2
+D_HALVES = D // K_PASS
+B_TILES = B // P
+U_HALVES = U // P
+WORDS = B * PACK
+
+FLOPS = 2 * B * (D + D * NB) * L * U + 2 * B * (1 + L) * U * U
+
+
+def regroup(engine_copy, dst, src):
+    engine_copy(
+        out=dst.rearrange("p (c i) t -> p c t i", i=4),
+        in_=src.rearrange("p t (c i) -> p c t i", i=4),
+    )
+
+
+def tile_tkancell_pa_kernel(
+    tc, x, lstm_out, kan_base_w, kan_spline_w, combine_w, combine_b, out
+):
+    nc = tc.nc
+    with ExitStack() as ctx:
+        keep = ctx.enter_context(tc.tile_pool(name="keep", bufs=1))
+        raw_pool = ctx.enter_context(tc.tile_pool(name="raw", bufs=3))
+        stage = ctx.enter_context(tc.tile_pool(name="stage", bufs=2))
+        acc_pool = ctx.enter_context(tc.psum_pool(name="acc", bufs=1))
+        small = ctx.enter_context(tc.psum_pool(name="small", bufs=2))
+
+        copiers = [nc.vector.tensor_copy, nc.scalar.copy]
+
+        x_sb = keep.tile([P, B_TILES, D], BF16)
+        nc.sync.dma_start(out=x_sb[:], in_=x.rearrange("(n p) d -> p n d", p=P))
+        lstm_sb = keep.tile([P, B_TILES, U], BF16)
+        nc.sync.dma_start(out=lstm_sb[:], in_=lstm_out.rearrange("(n p) u -> p n u", p=P))
+
+        ident = keep.tile([P, P], BF16)
+        make_identity(nc, ident[:])
+
+        xT = keep.tile([P, D_HALVES, B, PACK], BF16)
+        for g in range(D_HALVES):
+            for n in range(B_TILES):
+                xt = small.tile([P, PACK, P], BF16, tag="small")
+                for t in range(PACK):
+                    first = g * K_PASS + t * P
+                    nc.tensor.transpose(xt[:, t, :], x_sb[:, n, first : first + P], ident[:])
+                copiers[n % 2](
+                    out=xT[:, g, n * P : (n + 1) * P, :], in_=xt[:].rearrange("p t r -> p r t")
+                )
+
+        planes = keep.tile([P, 2, PACK, B], BF16)
+        for n in range(B_TILES):
+            lt = small.tile([P, U_HALVES, P], BF16, tag="small")
+            for h in range(U_HALVES):
+                nc.tensor.transpose(lt[:, h, :], lstm_sb[:, n, h * P : (h + 1) * P], ident[:])
+            copiers[n % 2](out=planes[:, 0, 0:U_HALVES, n * P : (n + 1) * P], in_=lt[:])
+
+        xc = keep.tile([P, D_HALVES, B, PACK], BF16)
+        nc.vector.tensor_scalar(
+            out=xc[:], in0=xT[:], scalar1=-4.0, scalar2=4.0, op0=ALU.max, op1=ALU.min
+        )
+
+        acc = {}
+        for l in range(L):
+            for h in range(U_HALVES):
+                acc[(l, h)] = acc_pool.tile([P, B], F32, name="acc_%d_%d" % (l, h))
+
+        def silu_pair():
+            acts = stage.tile([P, 2, WORDS], BF16, align_bytes=64, tag="acts")
+            for g in range(D_HALVES):
+                nc.scalar.activation(
+                    out=acts[:, g, :], in_=xT[:, g].rearrange("p b t -> p (b t)"), func=ACT.Silu
+                )
+            return acts
+
+        def basis_pair(g, t):
+            xg = xc[:, g].rearrange("p b t -> p (b t)")
+            fold = stage.tile([P, WORDS], F32, tag="fold")
+            nc.scalar.activation(out=fold[:], in_=xg, func=ACT.Abs, scale=2.5, bias=1.5 - t)
+            nc.scalar.activation(out=fold[:], in_=fold[:], func=ACT.Abs, bias=-2.0)
+            half_r2 = stage.tile([P, WORDS], F32, tag="half_r2")
+            nc.scalar.activation(out=half_r2[:], in_=fold[:], func=ACT.Square, scale=math.sqrt(0.5))
+            nc.scalar.activation(out=fold[:], in_=fold[:], func=ACT.Relu, scale=-1.0, bias=2.0)
+            sixth_a2 = stage.tile([P, WORDS], F32, tag="sixth_a2")
+            nc.scalar.activation(
+                out=sixth_a2[:], in_=fold[:], func=ACT.Square, scale=math.sqrt(1.0 / 6.0)
+            )
+            nc.vector.tensor_mul(out=half_r2[:], in0=fold[:], in1=half_r2[:])
+            nc.vector.scalar_tensor_tensor(
+                out=sixth_a2[:], in0=fold[:], scalar=-1.0, in1=sixth_a2[:], op0=ALU.mult, op1=ALU.mult
+            )
+            signed = stage.tile([P, WORDS], BF16, tag="signed")
+            nc.vector.scalar_tensor_tensor(
+                out=signed[:], in0=half_r2[:], scalar=2.0 / 3.0, in1=sixth_a2[:],
+                op0=ALU.subtract, op1=ALU.max,
+            )
+            side = stage.tile([P, WORDS], BF16, tag="side")
+            nc.vector.tensor_scalar(
+                out=side[:], in0=xg, scalar1=0.4 * t - 0.6, scalar2=0.5, op0=ALU.is_ge, op1=ALU.subtract
+            )
+            nc.vector.tensor_mul(out=signed[:], in0=signed[:], in1=side[:])
+            acts = stage.tile([P, 2, WORDS], BF16, align_bytes=64, tag="acts")
+            nc.vector.tensor_scalar(
+                out=acts[:, 0, :], in0=signed[:], scalar1=2.0, scalar2=0.0, op0=ALU.mult, op1=ALU.max
+            )
+            nc.vector.tensor_scalar(
+                out=acts[:, 1, :], in0=signed[:], scalar1=-2.0, scalar2=0.0, op0=ALU.mult, op1=ALU.max
+            )
+            return acts
+
+        base_rows = kan_base_w.rearrange("l (g t p) u -> l g p t u", g=D_HALVES, t=PACK, p=P)
+        spline_rows = kan_spline_w.rearrange(
+            "l (g t p k) u -> l g k p t u", g=D_HALVES, t=PACK, p=P, k=NB
+        )
+
+        steps = [("silu", 0, 0)] + [
+            ("basis", g, t) for g in range(D_HALVES) for t in range(FOLD)
+        ]
+        for step, (kind, g, t) in enumerate(steps):
+            w_raw = raw_pool.tile([P, L, 2, PACK, U], BF16)
+            for l in range(L):
+                for s in range(2):
+                    rows = base_rows[l, s] if kind == "silu" else spline_rows[l, g, t + s * FOLD]
+                    nc.sync.dma_start(out=w_raw[:, l, s], in_=rows)
+
+            acts = silu_pair() if kind == "silu" else basis_pair(g, t)
+            a_codes = stage.tile([P, 2, B], U32, align_bytes=64, tag="a_codes")
+            a_scales = stage.tile([P, 2, B], U8, align_bytes=64, tag="a_scales")
+            nc.vector.quantize_mx(
+                out=a_codes[:].rearrange("p s b -> p (s b)").bitcast(FP8X4),
+                scales=a_scales[:].rearrange("p s b -> p (s b)"),
+                in_=acts[:].rearrange("p s w -> p (s w)"),
+            )
+
+            w_grouped = stage.tile([P, L, 2, U, PACK], BF16, align_bytes=64, tag="w_grouped")
+            w_codes = stage.tile([P, L, 2, U], U32, align_bytes=64, tag="w_codes")
+            w_scales = stage.tile([P, L, 2, U], U8, align_bytes=64, tag="w_scales")
+            for l in range(L):
+                for s in range(2):
+                    regroup(copiers[(2 * l + s) % 2], w_grouped[:, l, s], w_raw[:, l, s])
+            for l in range(L):
+                nc.vector.quantize_mx(
+                    out=w_codes[:, l].rearrange("p s u -> p (s u)").bitcast(FP8X4),
+                    scales=w_scales[:, l].rearrange("p s u -> p (s u)"),
+                    in_=w_grouped[:, l].rearrange("p s u t -> p (s u t)"),
+                )
+
+            for s in range(2):
+                for l in range(L):
+                    for h in range(U_HALVES):
+                        cols = slice(h * P, (h + 1) * P)
+                        nc.tensor.matmul_mx(
+                            out=acc[(l, h)][:],
+                            lhsT=w_codes[:, l, s, cols].bitcast(FP8X4),
+                            lhsT_scale=w_scales[:, l, s, cols],
+                            rhs=a_codes[:, s, :].bitcast(FP8X4),
+                            rhs_scale=a_scales[:, s, :],
+                            start=(step == 0 and s == 0),
+                            stop=(step == len(steps) - 1 and s == 1),
+                        )
+
+        c_raw = keep.tile([P, 2, PACK, U], BF16)
+        nc.sync.dma_start(
+            out=c_raw[:].rearrange("p g t u -> p (g t) u"),
+            in_=combine_w.rearrange("(q p) u -> p q u", p=P),
+        )
+        bias_sb = keep.tile([P, U], BF16)
+        nc.sync.dma_start(out=bias_sb[:], in_=combine_b.partition_broadcast(P))
+        c_grouped = keep.tile([P, 2, U, PACK], BF16, align_bytes=64)
+        for G in range(2):
+            regroup(copiers[G], c_grouped[:, G], c_raw[:, G])
+        c_codes = keep.tile([P, 2, U], U32, align_bytes=64)
+        c_scales = keep.tile([P, 2, U], U8, align_bytes=64)
+        nc.vector.quantize_mx(
+            out=c_codes[:].rearrange("p g u -> p (g u)").bitcast(FP8X4),
+            scales=c_scales[:].rearrange("p g u -> p (g u)"),
+            in_=c_grouped[:].rearrange("p g u t -> p (g u t)"),
+        )
+
+        for l in range(L):
+            for h in range(U_HALVES):
+                plane = U_HALVES + l * U_HALVES + h
+                copiers[plane % 2](out=planes[:, plane // PACK, plane % PACK, :], in_=acc[(l, h)][:])
+        f_grouped = keep.tile([P, 2, B, PACK], BF16, align_bytes=64)
+        f_codes = keep.tile([P, 2, B], U32, align_bytes=64)
+        f_scales = keep.tile([P, 2, B], U8, align_bytes=64)
+        for G in range(2):
+            regroup(copiers[G], f_grouped[:, G], planes[:, G])
+        for G in range(2):
+            nc.vector.quantize_mx(
+                out=f_codes[:, G, :].bitcast(FP8X4),
+                scales=f_scales[:, G, :],
+                in_=f_grouped[:, G].rearrange("p b t -> p (b t)"),
+            )
+
+        result = keep.tile([P, B_TILES, U], F32)
+        out_rows = out.rearrange("(n p) u -> p n u", p=P)
+        for n in range(B_TILES):
+            rows = slice(n * P, (n + 1) * P)
+            proj = small.tile([P, U], F32, tag="small")
+            for G in range(2):
+                nc.tensor.matmul_mx(
+                    out=proj[:],
+                    lhsT=f_codes[:, G, rows].bitcast(FP8X4),
+                    lhsT_scale=f_scales[:, G, rows],
+                    rhs=c_codes[:, G, :].bitcast(FP8X4),
+                    rhs_scale=c_scales[:, G, :],
+                    start=(G == 0),
+                    stop=(G == 1),
+                )
+            nc.vector.tensor_add(out=result[:, n, :], in0=proj[:], in1=bias_sb[:])
+            nc.sync.dma_start(out=out_rows[:, n, :], in_=result[:, n, :])

@@ -26,191 +26,291 @@ WORDS = B * PACK
 FLOPS = 2 * B * (D + D * NB) * L * U + 2 * B * (1 + L) * U * U
 
 
-def regroup(engine_copy, dst, src):
-    engine_copy(
-        out=dst.rearrange("p (c i) t -> p c t i", i=4),
-        in_=src.rearrange("p t (c i) -> p c t i", i=4),
-    )
-
-
 def tile_tkancell_pa_kernel(
     tc, x, lstm_out, kan_base_w, kan_spline_w, combine_w, combine_b, out
 ):
     nc = tc.nc
     with ExitStack() as ctx:
         keep = ctx.enter_context(tc.tile_pool(name="keep", bufs=1))
-        raw_pool = ctx.enter_context(tc.tile_pool(name="raw", bufs=3))
-        stage = ctx.enter_context(tc.tile_pool(name="stage", bufs=2))
+        raw_pool = ctx.enter_context(tc.tile_pool(name="raw", bufs=4))
+        grouped_pool = ctx.enter_context(tc.tile_pool(name="grouped", bufs=4))
+        w_pool = ctx.enter_context(tc.tile_pool(name="w", bufs=2))
+        stage = ctx.enter_context(tc.tile_pool(name="stage", bufs=1))
+        wide = ctx.enter_context(tc.tile_pool(name="wide", bufs=3))
+        square_pool = ctx.enter_context(tc.tile_pool(name="squares", bufs=4))
+        core_pool = ctx.enter_context(tc.tile_pool(name="cores", bufs=1))
         acc_pool = ctx.enter_context(tc.psum_pool(name="acc", bufs=1))
         small = ctx.enter_context(tc.psum_pool(name="small", bufs=2))
 
-        copiers = [nc.vector.tensor_copy, nc.scalar.copy]
-
-        x_sb = keep.tile([P, B_TILES, D], BF16)
-        nc.sync.dma_start(out=x_sb[:], in_=x.rearrange("(n p) d -> p n d", p=P))
-        lstm_sb = keep.tile([P, B_TILES, U], BF16)
-        nc.sync.dma_start(out=lstm_sb[:], in_=lstm_out.rearrange("(n p) u -> p n u", p=P))
+        on_vector = nc.vector.tensor_copy
+        on_scalar = nc.scalar.copy
+        copiers = [on_vector, on_scalar]
 
         ident = keep.tile([P, P], BF16)
         make_identity(nc, ident[:])
+        ident_words = keep.tile([P, P], F32)
+        make_identity(nc, ident_words[:])
+        ctx.enter_context(tc.manual_schedule())
 
-        xT = keep.tile([P, D_HALVES, B, PACK], BF16)
-        for g in range(D_HALVES):
-            for n in range(B_TILES):
-                xt = small.tile([P, PACK, P], BF16, tag="small")
-                for t in range(PACK):
-                    first = g * K_PASS + t * P
-                    nc.tensor.transpose(xt[:, t, :], x_sb[:, n, first : first + P], ident[:])
-                copiers[n % 2](
-                    out=xT[:, g, n * P : (n + 1) * P, :], in_=xt[:].rearrange("p t r -> p r t")
-                )
-
-        planes = keep.tile([P, 2, PACK, B], BF16)
+        x_sb = square_pool.tile([P, B_TILES, D], BF16, align_bytes=64, tag="sq")
+        x_rows = x.rearrange("(n p) d -> p n d", p=P)
         for n in range(B_TILES):
-            lt = small.tile([P, U_HALVES, P], BF16, tag="small")
-            for h in range(U_HALVES):
-                nc.tensor.transpose(lt[:, h, :], lstm_sb[:, n, h * P : (h + 1) * P], ident[:])
-            copiers[n % 2](out=planes[:, 0, 0:U_HALVES, n * P : (n + 1) * P], in_=lt[:])
+            nc.sync.dma_start(out=x_sb[:, n, :], in_=x_rows[:, n, :])
 
-        xc = keep.tile([P, D_HALVES, B, PACK], BF16)
-        nc.vector.tensor_scalar(
-            out=xc[:], in0=xT[:], scalar1=-4.0, scalar2=4.0, op0=ALU.max, op1=ALU.min
+        steps = [("basis", g, t) for g in range(D_HALVES) for t in range(FOLD)]
+        steps.insert(1, ("silu", 0, 0))
+        a_codes = keep.tile([P, len(steps), 2, B], U32, align_bytes=64)
+        a_scales = keep.tile([P, len(steps), 2, B], U8, align_bytes=64)
+
+        units = [[(step, 0), (step, 1)] for step in range(len(steps))]
+        thirds = [[(step, 2) for step in range(first, min(first + 2, len(steps)))] for first in range(0, len(steps), 2)]
+        units = units[:7] + thirds[:1] + units[7:8] + thirds[1:2] + units[8:] + thirds[2:]
+        vector_columns = [1024] * 3 + [256] * 4 + [128] * 5 + [256] * 2
+
+        base_rows = kan_base_w.rearrange("l (g p t) u -> l g p t u", g=D_HALVES, t=PACK, p=P)
+        spline_rows = kan_spline_w.rearrange(
+            "l (g p t k) u -> l g k p t u", g=D_HALVES, t=PACK, p=P, k=NB
         )
+        raws, grouped, coded = {}, {}, {}
+
+        def load(k):
+            raw = raw_pool.tile([P, PACK, 4, U], BF16, tag="raw")
+            for i, (step, l) in enumerate(units[k]):
+                kind, g, t = steps[step]
+                for s in range(2):
+                    rows = base_rows[l, s] if kind == "silu" else spline_rows[l, g, t + s * FOLD]
+                    nc.sync.dma_start(out=raw[:, :, 2 * i + s, :], in_=rows)
+            raws[k] = raw
+
+        def lay_out(k):
+            w_grouped = grouped_pool.tile([P, 4 * U, PACK], BF16, align_bytes=64, tag="w_grouped")
+            columns = 2 * U * len(units[k])
+            rows = raws.pop(k)[:].rearrange("p t q u -> p t (q u)")
+            cut = vector_columns[k]
+            for copy, first, last in ((on_vector, 0, cut), (on_scalar, cut, columns)):
+                if last > first:
+                    copy(
+                        out=w_grouped[:, first:last, :].rearrange("p (c i) t -> p c t i", i=4),
+                        in_=rows[:, :, first:last].rearrange("p t (c i) -> p c t i", i=4),
+                    )
+            grouped[k] = w_grouped
+
+        def quantize_weights(k):
+            w_codes = w_pool.tile([P, 4, U], U32, align_bytes=64, tag="w_codes")
+            w_scales = w_pool.tile([P, 4, U], U8, align_bytes=64, tag="w_scales")
+            passes = 2 * len(units[k])
+            nc.vector.quantize_mx(
+                out=w_codes[:, :passes].rearrange("p q u -> p (q u)").bitcast(FP8X4),
+                scales=w_scales[:, :passes].rearrange("p q u -> p (q u)"),
+                in_=grouped.pop(k)[:, : passes * U].rearrange("p c t -> p (c t)"),
+            )
+            coded[k] = w_codes, w_scales
 
         acc = {}
         for l in range(L):
             for h in range(U_HALVES):
                 acc[(l, h)] = acc_pool.tile([P, B], F32, name="acc_%d_%d" % (l, h))
 
-        def silu_pair():
-            acts = stage.tile([P, 2, WORDS], BF16, align_bytes=64, tag="acts")
-            for g in range(D_HALVES):
-                nc.scalar.activation(
-                    out=acts[:, g, :], in_=xT[:, g].rearrange("p b t -> p (b t)"), func=ACT.Silu
-                )
-            return acts
-
-        def basis_pair(g, t):
-            xg = xc[:, g].rearrange("p b t -> p (b t)")
-            fold = stage.tile([P, WORDS], F32, tag="fold")
-            nc.scalar.activation(out=fold[:], in_=xg, func=ACT.Abs, scale=2.5, bias=1.5 - t)
-            nc.scalar.activation(out=fold[:], in_=fold[:], func=ACT.Abs, bias=-2.0)
-            half_r2 = stage.tile([P, WORDS], F32, tag="half_r2")
-            nc.scalar.activation(out=half_r2[:], in_=fold[:], func=ACT.Square, scale=math.sqrt(0.5))
-            nc.scalar.activation(out=fold[:], in_=fold[:], func=ACT.Relu, scale=-1.0, bias=2.0)
-            sixth_a2 = stage.tile([P, WORDS], F32, tag="sixth_a2")
-            nc.scalar.activation(
-                out=sixth_a2[:], in_=fold[:], func=ACT.Square, scale=math.sqrt(1.0 / 6.0)
-            )
-            nc.vector.tensor_mul(out=half_r2[:], in0=fold[:], in1=half_r2[:])
-            nc.vector.scalar_tensor_tensor(
-                out=sixth_a2[:], in0=fold[:], scalar=-1.0, in1=sixth_a2[:], op0=ALU.mult, op1=ALU.mult
-            )
-            signed = stage.tile([P, WORDS], BF16, tag="signed")
-            nc.vector.scalar_tensor_tensor(
-                out=signed[:], in0=half_r2[:], scalar=2.0 / 3.0, in1=sixth_a2[:],
-                op0=ALU.subtract, op1=ALU.max,
-            )
-            side = stage.tile([P, WORDS], BF16, tag="side")
-            nc.vector.tensor_scalar(
-                out=side[:], in0=xg, scalar1=0.4 * t - 0.6, scalar2=0.5, op0=ALU.is_ge, op1=ALU.subtract
-            )
-            nc.vector.tensor_mul(out=signed[:], in0=signed[:], in1=side[:])
-            acts = stage.tile([P, 2, WORDS], BF16, align_bytes=64, tag="acts")
-            nc.vector.tensor_scalar(
-                out=acts[:, 0, :], in0=signed[:], scalar1=2.0, scalar2=0.0, op0=ALU.mult, op1=ALU.max
-            )
-            nc.vector.tensor_scalar(
-                out=acts[:, 1, :], in0=signed[:], scalar1=-2.0, scalar2=0.0, op0=ALU.mult, op1=ALU.max
-            )
-            return acts
-
-        base_rows = kan_base_w.rearrange("l (g t p) u -> l g p t u", g=D_HALVES, t=PACK, p=P)
-        spline_rows = kan_spline_w.rearrange(
-            "l (g t p k) u -> l g k p t u", g=D_HALVES, t=PACK, p=P, k=NB
-        )
-
-        steps = [("silu", 0, 0)] + [
-            ("basis", g, t) for g in range(D_HALVES) for t in range(FOLD)
-        ]
-        for step, (kind, g, t) in enumerate(steps):
-            w_raw = raw_pool.tile([P, L, 2, PACK, U], BF16)
-            for l in range(L):
+        def multiply(k):
+            w_codes, w_scales = coded.pop(k)
+            for i, (step, l) in enumerate(units[k]):
                 for s in range(2):
-                    rows = base_rows[l, s] if kind == "silu" else spline_rows[l, g, t + s * FOLD]
-                    nc.sync.dma_start(out=w_raw[:, l, s], in_=rows)
-
-            acts = silu_pair() if kind == "silu" else basis_pair(g, t)
-            a_codes = stage.tile([P, 2, B], U32, align_bytes=64, tag="a_codes")
-            a_scales = stage.tile([P, 2, B], U8, align_bytes=64, tag="a_scales")
-            nc.vector.quantize_mx(
-                out=a_codes[:].rearrange("p s b -> p (s b)").bitcast(FP8X4),
-                scales=a_scales[:].rearrange("p s b -> p (s b)"),
-                in_=acts[:].rearrange("p s w -> p (s w)"),
-            )
-
-            w_grouped = stage.tile([P, L, 2, U, PACK], BF16, align_bytes=64, tag="w_grouped")
-            w_codes = stage.tile([P, L, 2, U], U32, align_bytes=64, tag="w_codes")
-            w_scales = stage.tile([P, L, 2, U], U8, align_bytes=64, tag="w_scales")
-            for l in range(L):
-                for s in range(2):
-                    regroup(copiers[(2 * l + s) % 2], w_grouped[:, l, s], w_raw[:, l, s])
-            for l in range(L):
-                nc.vector.quantize_mx(
-                    out=w_codes[:, l].rearrange("p s u -> p (s u)").bitcast(FP8X4),
-                    scales=w_scales[:, l].rearrange("p s u -> p (s u)"),
-                    in_=w_grouped[:, l].rearrange("p s u t -> p (s u t)"),
-                )
-
-            for s in range(2):
-                for l in range(L):
                     for h in range(U_HALVES):
                         cols = slice(h * P, (h + 1) * P)
                         nc.tensor.matmul_mx(
                             out=acc[(l, h)][:],
-                            lhsT=w_codes[:, l, s, cols].bitcast(FP8X4),
-                            lhsT_scale=w_scales[:, l, s, cols],
-                            rhs=a_codes[:, s, :].bitcast(FP8X4),
-                            rhs_scale=a_scales[:, s, :],
+                            lhsT=w_codes[:, 2 * i + s, cols].bitcast(FP8X4),
+                            lhsT_scale=w_scales[:, 2 * i + s, cols],
+                            rhs=a_codes[:, step, s, :].bitcast(FP8X4),
+                            rhs_scale=a_scales[:, step, s, :],
                             start=(step == 0 and s == 0),
                             stop=(step == len(steps) - 1 and s == 1),
                         )
 
-        c_raw = keep.tile([P, 2, PACK, U], BF16)
-        nc.sync.dma_start(
-            out=c_raw[:].rearrange("p g t u -> p (g t) u"),
-            in_=combine_w.rearrange("(q p) u -> p q u", p=P),
-        )
-        bias_sb = keep.tile([P, U], BF16)
-        nc.sync.dma_start(out=bias_sb[:], in_=combine_b.partition_broadcast(P))
-        c_grouped = keep.tile([P, 2, U, PACK], BF16, align_bytes=64)
-        for G in range(2):
-            regroup(copiers[G], c_grouped[:, G], c_raw[:, G])
-        c_codes = keep.tile([P, 2, U], U32, align_bytes=64)
-        c_scales = keep.tile([P, 2, U], U8, align_bytes=64)
-        nc.vector.quantize_mx(
-            out=c_codes[:].rearrange("p g u -> p (g u)").bitcast(FP8X4),
-            scales=c_scales[:].rearrange("p g u -> p (g u)"),
-            in_=c_grouped[:].rearrange("p g u t -> p (g u t)"),
-        )
+        xT = keep.tile([P, D_HALVES, B, PACK], BF16)
+        x_words = x_sb[:].bitcast(F32)
+        xT_words = xT[:].bitcast(F32)
 
-        for l in range(L):
-            for h in range(U_HALVES):
-                plane = U_HALVES + l * U_HALVES + h
-                copiers[plane % 2](out=planes[:, plane // PACK, plane % PACK, :], in_=acc[(l, h)][:])
-        f_grouped = keep.tile([P, 2, B, PACK], BF16, align_bytes=64)
-        f_codes = keep.tile([P, 2, B], U32, align_bytes=64)
-        f_scales = keep.tile([P, 2, B], U8, align_bytes=64)
-        for G in range(2):
-            regroup(copiers[G], f_grouped[:, G], planes[:, G])
-        for G in range(2):
-            nc.vector.quantize_mx(
-                out=f_codes[:, G, :].bitcast(FP8X4),
-                scales=f_scales[:, G, :],
-                in_=f_grouped[:, G].rearrange("p b t -> p (b t)"),
+        def transpose_x(n):
+            xt = small.tile([P, D_HALVES, 2, P], F32, tag="small")
+            for g in range(D_HALVES):
+                for u in range(2):
+                    first = g * (K_PASS // 2) + u
+                    nc.tensor.transpose(
+                        xt[:, g, u, :], x_words[:, n, first : (g + 1) * (K_PASS // 2) : 2], ident_words[:]
+                    )
+            copiers[n % 2](
+                out=xT_words[:, :, n * P : (n + 1) * P, :], in_=xt[:].rearrange("p g u r -> p g r u")
             )
 
-        result = keep.tile([P, B_TILES, U], F32)
+        def distances(step):
+            kind, g, t = steps[step]
+            if kind == "silu":
+                acts = square_pool.tile([P, 2, WORDS], BF16, align_bytes=64, tag="sq")
+                for g in range(D_HALVES):
+                    nc.scalar.activation(
+                        out=acts[:, g, :], in_=xT[:, g].rearrange("p b t -> p (b t)"), func=ACT.Silu
+                    )
+                return acts
+            r = wide.tile([P, WORDS], F32, tag="dist")
+            xg = xT[:, g].rearrange("p b t -> p (b t)")
+            nc.scalar.activation(out=r[:], in_=xg, func=ACT.Abs, scale=2.5, bias=1.5 - t)
+            nc.scalar.activation(out=r[:], in_=r[:], func=ACT.Abs, bias=-2.0)
+            sq = square_pool.tile([P, WORDS], F32, align_bytes=64, tag="sq")
+            nc.scalar.activation(
+                out=sq[:], in_=r[:], func=ACT.Square, scale=-math.sqrt(1.0 / 6.0), bias=2.0 * math.sqrt(1.0 / 6.0)
+            )
+            if t > 0:
+                return r, sq
+            e = wide.tile([P, WORDS], F32, tag="dist")
+            nc.scalar.activation(out=e[:], in_=r[:], func=ACT.Abs, scale=-1.0, bias=2.0)
+            nc.scalar.activation(out=e[:], in_=e[:], func=ACT.Abs, bias=-1.0)
+            core_squares = []
+            for scale, bias in ((-1.0, 1.0), (1.0, 0.0)):
+                core_sq = square_pool.tile([P, WORDS], F32, align_bytes=64, tag="sq")
+                nc.scalar.activation(out=core_sq[:], in_=e[:], func=ACT.Square, scale=scale, bias=bias)
+                core_squares.append(core_sq)
+            return r, sq, e, core_squares
+
+        neg_k = {}
+
+        def bases(step, parts):
+            kind, g, t = steps[step]
+            if kind == "silu":
+                return parts
+            r, sq = parts[:2]
+            bump = stage.tile([P, WORDS], BF16, tag="bump")
+            nc.vector.scalar_tensor_tensor(
+                out=bump[:], in0=r[:], scalar=2.0, in1=sq[:], op0=ALU.subtract, op1=ALU.mult
+            )
+            if t == 0:
+                e, core_squares = parts[2:]
+                for odd, shift, half in ((0, 1.0, 0.5), (1, -2.0, -0.5)):
+                    core_sq = core_squares[odd]
+                    nc.vector.scalar_tensor_tensor(
+                        out=core_sq[:], in0=e[:], scalar=shift, in1=core_sq[:], op0=ALU.add, op1=ALU.mult
+                    )
+                    neg_k[odd] = core_pool.tile([P, WORDS], BF16, name="neg_k%d" % odd)
+                    nc.vector.tensor_scalar(
+                        out=neg_k[odd][:], in0=core_sq[:], scalar1=half, scalar2=2.0 / 3.0,
+                        op0=ALU.mult, op1=ALU.subtract,
+                    )
+            nc.vector.tensor_max(out=bump[:], in0=bump[:], in1=neg_k[t % 2][:])
+            nc.vector.tensor_scalar(
+                out=bump[:], in0=bump[:], scalar1=-1.0, scalar2=0.0, op0=ALU.mult, op1=ALU.max
+            )
+            left = stage.tile([P, WORDS], BF16, tag="left")
+            nc.vector.tensor_single_scalar(
+                out=left[:], in_=xT[:, g].rearrange("p b t -> p (b t)"), scalar=0.4 * t - 0.6, op=ALU.is_lt
+            )
+            acts = stage.tile([P, 2, WORDS], BF16, align_bytes=64, tag="acts")
+            nc.vector.tensor_mul(out=acts[:, 0, :], in0=bump[:], in1=left[:])
+            nc.vector.tensor_sub(out=acts[:, 1, :], in0=bump[:], in1=acts[:, 0, :])
+            return acts
+
+
+        def quantize_activations(step, acts):
+            nc.vector.quantize_mx(
+                out=a_codes[:, step].rearrange("p s b -> p (s b)").bitcast(FP8X4),
+                scales=a_scales[:, step].rearrange("p s b -> p (s b)"),
+                in_=acts[:].rearrange("p s w -> p (s w)"),
+            )
+
+        lstm_sb = keep.tile([P, B_TILES, U], BF16)
+        c_raw = keep.tile([P, 2, PACK, U], BF16)
+        bias_sb = keep.tile([P, U], BF16)
+        c_codes = keep.tile([P, 2, U], U32, align_bytes=64)
+        c_scales = keep.tile([P, 2, U], U8, align_bytes=64)
+        planes = keep.tile([P, 2, PACK, B], BF16)
+        f_codes = keep.tile([P, 2, B], U32, align_bytes=64)
+        f_scales = keep.tile([P, 2, B], U8, align_bytes=64)
+
+        def load_projection():
+            nc.sync.dma_start(out=lstm_sb[:], in_=lstm_out.rearrange("(n p) u -> p n u", p=P))
+            nc.sync.dma_start(
+                out=c_raw[:].rearrange("p g t u -> p (g t) u"),
+                in_=combine_w.rearrange("(q p) u -> p q u", p=P),
+            )
+            nc.sync.dma_start(out=bias_sb[:], in_=combine_b.partition_broadcast(P))
+
+        def transpose_lstm():
+            for n in range(B_TILES):
+                lt = small.tile([P, U_HALVES, P], BF16, tag="small")
+                for h in range(U_HALVES):
+                    nc.tensor.transpose(lt[:, h, :], lstm_sb[:, n, h * P : (h + 1) * P], ident[:])
+                copiers[n % 2](out=planes[:, 0, 0:U_HALVES, n * P : (n + 1) * P], in_=lt[:])
+
+        def quantize_projection():
+            c_grouped = grouped_pool.tile([P, 2, U, PACK], BF16, align_bytes=64, tag="w_grouped")
+            for G in range(2):
+                copiers[G](
+                    out=c_grouped[:, G].rearrange("p (c i) t -> p c t i", i=4),
+                    in_=c_raw[:, G].rearrange("p t (c i) -> p c t i", i=4),
+                )
+            nc.vector.quantize_mx(
+                out=c_codes[:].rearrange("p g u -> p (g u)").bitcast(FP8X4),
+                scales=c_scales[:].rearrange("p g u -> p (g u)"),
+                in_=c_grouped[:].rearrange("p g u t -> p (g u t)"),
+            )
+
+        def copy_out(l):
+            for h in range(U_HALVES):
+                plane = U_HALVES + l * U_HALVES + h
+                copiers[h](out=planes[:, plane // PACK, plane % PACK, :], in_=acc[(l, h)][:])
+
+        def quantize_combined(G):
+            f_grouped = square_pool.tile([P, B, PACK], BF16, align_bytes=64, tag="sq")
+            for i in range(2):
+                rows = slice(i * B // 2, (i + 1) * B // 2)
+                copiers[i](
+                    out=f_grouped[:, rows].rearrange("p (c i) t -> p c t i", i=4),
+                    in_=planes[:, G, :, rows].rearrange("p t (c i) -> p c t i", i=4),
+                )
+            for i in range(2):
+                rows = slice(i * B // 2, (i + 1) * B // 2)
+                nc.vector.quantize_mx(
+                    out=f_codes[:, G, rows].bitcast(FP8X4),
+                    scales=f_scales[:, G, rows],
+                    in_=f_grouped[:, rows].rearrange("p b t -> p (b t)"),
+                )
+
+        for k in range(4):
+            load(k)
+        for n in range(B_TILES):
+            transpose_x(n)
+        parts = distances(0)
+        lay_out(0)
+        quantize_weights(0)
+        lay_out(1)
+        lay_out(2)
+        for k in range(len(units)):
+            if k + 4 < len(units):
+                load(k + 4)
+            if k == 0:
+                load_projection()
+            step, l = units[k][0]
+            if l == 0:
+                ahead = distances(step + 1) if step + 1 < len(steps) else None
+                quantize_activations(step, bases(step, parts))
+                parts = ahead
+            if k == 2:
+                transpose_lstm()
+            if k == 11:
+                quantize_projection()
+            if k + 3 < len(units):
+                lay_out(k + 3)
+            if k + 1 < len(units):
+                quantize_weights(k + 1)
+            multiply(k)
+            if k == len(units) - 3:
+                copy_out(0)
+                copy_out(1)
+            if k == len(units) - 2:
+                quantize_combined(0)
+        copy_out(L - 1)
+        quantize_combined(1)
+
+        result = stage.tile([P, B_TILES, U], F32, align_bytes=64, tag="acts")
         out_rows = out.rearrange("(n p) u -> p n u", p=P)
         for n in range(B_TILES):
             rows = slice(n * P, (n + 1) * P)

@@ -26,6 +26,13 @@ WORDS = B * PACK
 FLOPS = 2 * B * (D + D * NB) * L * U + 2 * B * (1 + L) * U * U
 
 
+def weave(main, fill):
+    for i in range(max(len(main), len(fill))):
+        for calls in (main, fill):
+            if i < len(calls):
+                calls[i]()
+
+
 def tile_tkancell_pa_kernel(
     tc, x, lstm_out, kan_base_w, kan_spline_w, combine_w, combine_b, out
 ):
@@ -36,9 +43,9 @@ def tile_tkancell_pa_kernel(
         grouped_pool = ctx.enter_context(tc.tile_pool(name="grouped", bufs=4))
         w_pool = ctx.enter_context(tc.tile_pool(name="w", bufs=2))
         stage = ctx.enter_context(tc.tile_pool(name="stage", bufs=1))
+        left_pool = ctx.enter_context(tc.tile_pool(name="left", bufs=2))
         wide = ctx.enter_context(tc.tile_pool(name="wide", bufs=3))
         square_pool = ctx.enter_context(tc.tile_pool(name="squares", bufs=4))
-        core_pool = ctx.enter_context(tc.tile_pool(name="cores", bufs=1))
         acc_pool = ctx.enter_context(tc.psum_pool(name="acc", bufs=1))
         small = ctx.enter_context(tc.psum_pool(name="small", bufs=2))
 
@@ -52,7 +59,7 @@ def tile_tkancell_pa_kernel(
         make_identity(nc, ident_words[:])
         ctx.enter_context(tc.manual_schedule())
 
-        x_sb = square_pool.tile([P, B_TILES, D], BF16, align_bytes=64, tag="sq")
+        x_sb = square_pool.tile([P, B_TILES, D], BF16, align_bytes=64, name="sq")
         x_rows = x.rearrange("(n p) d -> p n d", p=P)
         for n in range(B_TILES):
             nc.sync.dma_start(out=x_sb[:, n, :], in_=x_rows[:, n, :])
@@ -64,8 +71,7 @@ def tile_tkancell_pa_kernel(
 
         units = [[(step, 0), (step, 1)] for step in range(len(steps))]
         thirds = [[(step, 2) for step in range(first, min(first + 2, len(steps)))] for first in range(0, len(steps), 2)]
-        units = units[:7] + thirds[:1] + units[7:8] + thirds[1:2] + units[8:] + thirds[2:]
-        vector_columns = [1024] * 3 + [256] * 4 + [128] * 5 + [256] * 2
+        units = units[:8] + thirds[:1] + units[8:] + thirds[1:]
 
         base_rows = kan_base_w.rearrange("l (g p t) u -> l g p t u", g=D_HALVES, t=PACK, p=P)
         spline_rows = kan_spline_w.rearrange(
@@ -82,18 +88,53 @@ def tile_tkancell_pa_kernel(
                     nc.sync.dma_start(out=raw[:, :, 2 * i + s, :], in_=rows)
             raws[k] = raw
 
-        def lay_out(k):
-            w_grouped = grouped_pool.tile([P, 4 * U, PACK], BF16, align_bytes=64, tag="w_grouped")
+        def lay_out(k, copy, first, last):
+            if last <= first:
+                return
+            if k not in grouped:
+                grouped[k] = grouped_pool.tile([P, 4 * U, PACK], BF16, align_bytes=64, name="w_grouped")
+            rows = raws[k][:].rearrange("p t q u -> p t (q u)")
+            copy(
+                out=grouped[k][:, first:last, :].rearrange("p (c i) t -> p c t i", i=4),
+                in_=rows[:, :, first:last].rearrange("p t (c i) -> p c t i", i=4),
+            )
+
+        moves = [(k, q) for k in range(4, 9) for q in range(2 * len(units[k]))]
+        moved = {}
+
+        def move(i):
+            if i >= len(moves):
+                return
+            k, q = moves[i]
+            moved[i] = small.tile([P, U, PACK], BF16, name="small")
+            for t in range(0, PACK, 2):
+                nc.tensor.matmul(
+                    moved[i][:, :, t : t + 2].rearrange("p c t -> p t c"),
+                    lhsT=ident[:], rhs=raws[k][:, t : t + 2, q, :], start=True, stop=True,
+                )
+
+        def copy_moved(k, q):
+            i = moves.index((k, q))
+            if i == 0:
+                move(0)
+                move(1)
+            if k not in grouped:
+                grouped[k] = grouped_pool.tile([P, 4 * U, PACK], BF16, align_bytes=64, name="w_grouped")
+            on_scalar(out=grouped[k][:, q * U : (q + 1) * U, :], in_=moved[i][:])
+            move(i + 2)
+
+        def layout_calls(k):
+            if k >= len(units):
+                return [], []
             columns = 2 * U * len(units[k])
-            rows = raws.pop(k)[:].rearrange("p t q u -> p t (q u)")
-            cut = vector_columns[k]
-            for copy, first, last in ((on_vector, 0, cut), (on_scalar, cut, columns)):
-                if last > first:
-                    copy(
-                        out=w_grouped[:, first:last, :].rearrange("p (c i) t -> p c t i", i=4),
-                        in_=rows[:, :, first:last].rearrange("p t (c i) -> p c t i", i=4),
-                    )
-            grouped[k] = w_grouped
+            if 4 <= k < 9:
+                return [], [lambda q=q: copy_moved(k, q) for q in range(2 * len(units[k]))]
+            cut = min(1024 if k < 4 else 0, columns)
+            half = (cut + columns) // 32 * 16
+            return (
+                [lambda: lay_out(k, on_vector, 0, cut)],
+                [lambda: lay_out(k, on_scalar, cut, half), lambda: lay_out(k, on_scalar, half, columns)],
+            )
 
         def quantize_weights(k):
             w_codes = w_pool.tile([P, 4, U], U32, align_bytes=64, tag="w_codes")
@@ -102,17 +143,35 @@ def tile_tkancell_pa_kernel(
             nc.vector.quantize_mx(
                 out=w_codes[:, :passes].rearrange("p q u -> p (q u)").bitcast(FP8X4),
                 scales=w_scales[:, :passes].rearrange("p q u -> p (q u)"),
-                in_=grouped.pop(k)[:, : passes * U].rearrange("p c t -> p (c t)"),
+                in_=grouped[k][:, : passes * U].rearrange("p c t -> p (c t)"),
             )
             coded[k] = w_codes, w_scales
 
+        xT = keep.tile([P, D_HALVES, B, PACK], BF16)
+        x_words = x_sb[:].bitcast(F32)
+        xT_words = xT[:].bitcast(F32)
+
+        def transpose_x(n):
+            xt = acc_pool.tile([P, D_HALVES, 2, P], F32, name="acc_%d" % n)
+            for g in range(D_HALVES):
+                for u in range(2):
+                    first = g * (K_PASS // 2) + u
+                    nc.tensor.transpose(
+                        xt[:, g, u, :], x_words[:, n, first : (g + 1) * (K_PASS // 2) : 2], ident_words[:]
+                    )
+            copiers[n % 2](
+                out=xT_words[:, :, n * P : (n + 1) * P, :], in_=xt[:].rearrange("p g u r -> p g r u")
+            )
+
         acc = {}
-        for l in range(L):
-            for h in range(U_HALVES):
-                acc[(l, h)] = acc_pool.tile([P, B], F32, name="acc_%d_%d" % (l, h))
+
+        def open_accumulators():
+            for l in range(L):
+                for h in range(U_HALVES):
+                    acc[(l, h)] = acc_pool.tile([P, B], F32, name="acc_%d" % (U_HALVES * l + h))
 
         def multiply(k):
-            w_codes, w_scales = coded.pop(k)
+            w_codes, w_scales = coded[k]
             for i, (step, l) in enumerate(units[k]):
                 for s in range(2):
                     for h in range(U_HALVES):
@@ -127,93 +186,126 @@ def tile_tkancell_pa_kernel(
                             stop=(step == len(steps) - 1 and s == 1),
                         )
 
-        xT = keep.tile([P, D_HALVES, B, PACK], BF16)
-        x_words = x_sb[:].bitcast(F32)
-        xT_words = xT[:].bitcast(F32)
+        acts, lefts, distance, square, core, neg_k = {}, {}, {}, {}, {}, {}
 
-        def transpose_x(n):
-            xt = small.tile([P, D_HALVES, 2, P], F32, tag="small")
-            for g in range(D_HALVES):
-                for u in range(2):
-                    first = g * (K_PASS // 2) + u
-                    nc.tensor.transpose(
-                        xt[:, g, u, :], x_words[:, n, first : (g + 1) * (K_PASS // 2) : 2], ident_words[:]
-                    )
-            copiers[n % 2](
-                out=xT_words[:, :, n * P : (n + 1) * P, :], in_=xt[:].rearrange("p g u r -> p g r u")
-            )
+        def features(g):
+            return xT[:, g].rearrange("p b t -> p (b t)")
 
-        def distances(step):
+        def scalar_calls(step):
+            if step >= len(steps):
+                return []
             kind, g, t = steps[step]
-            if kind == "silu":
-                acts = square_pool.tile([P, 2, WORDS], BF16, align_bytes=64, tag="sq")
-                for g in range(D_HALVES):
-                    nc.scalar.activation(
-                        out=acts[:, g, :], in_=xT[:, g].rearrange("p b t -> p (b t)"), func=ACT.Silu
-                    )
-                return acts
-            r = wide.tile([P, WORDS], F32, tag="dist")
-            xg = xT[:, g].rearrange("p b t -> p (b t)")
-            nc.scalar.activation(out=r[:], in_=xg, func=ACT.Abs, scale=2.5, bias=1.5 - t)
-            nc.scalar.activation(out=r[:], in_=r[:], func=ACT.Abs, bias=-2.0)
-            sq = square_pool.tile([P, WORDS], F32, align_bytes=64, tag="sq")
-            nc.scalar.activation(
-                out=sq[:], in_=r[:], func=ACT.Square, scale=-math.sqrt(1.0 / 6.0), bias=2.0 * math.sqrt(1.0 / 6.0)
-            )
-            if t > 0:
-                return r, sq
-            e = wide.tile([P, WORDS], F32, tag="dist")
-            nc.scalar.activation(out=e[:], in_=r[:], func=ACT.Abs, scale=-1.0, bias=2.0)
-            nc.scalar.activation(out=e[:], in_=e[:], func=ACT.Abs, bias=-1.0)
-            core_squares = []
-            for scale, bias in ((-1.0, 1.0), (1.0, 0.0)):
-                core_sq = square_pool.tile([P, WORDS], F32, align_bytes=64, tag="sq")
-                nc.scalar.activation(out=core_sq[:], in_=e[:], func=ACT.Square, scale=scale, bias=bias)
-                core_squares.append(core_sq)
-            return r, sq, e, core_squares
 
-        neg_k = {}
+            def silu(half):
+                if half == 0:
+                    acts[step] = square_pool.tile([P, 2, WORDS], BF16, align_bytes=64, name="sq")
+                nc.scalar.activation(out=acts[step][:, half, :], in_=features(half), func=ACT.Silu)
 
-        def bases(step, parts):
-            kind, g, t = steps[step]
+            def fold():
+                distance[step] = wide.tile([P, WORDS], F32, name="dist")
+                nc.scalar.activation(
+                    out=distance[step][:], in_=features(g), func=ACT.Abs, scale=2.5, bias=1.5 - t
+                )
+
+            def from_centre():
+                nc.scalar.activation(
+                    out=distance[step][:], in_=distance[step][:], func=ACT.Abs, bias=-2.0
+                )
+
+            def tail_square():
+                square[step] = square_pool.tile([P, WORDS], F32, align_bytes=64, name="sq")
+                nc.scalar.activation(
+                    out=square[step][:], in_=distance[step][:], func=ACT.Square,
+                    scale=-math.sqrt(1.0 / 6.0), bias=2.0 * math.sqrt(1.0 / 6.0),
+                )
+
+            def from_even_bump():
+                core[0] = wide.tile([P, WORDS], F32, name="dist")
+                nc.scalar.activation(
+                    out=core[0][:], in_=distance[step][:], func=ACT.Abs, scale=-1.0, bias=2.0
+                )
+
+            def from_odd_knot():
+                nc.scalar.activation(out=core[0][:], in_=core[0][:], func=ACT.Abs, bias=-1.0)
+
+            def core_square(odd):
+                core[1 + odd] = square_pool.tile([P, WORDS], F32, align_bytes=64, name="sq")
+                nc.scalar.activation(
+                    out=core[1 + odd][:], in_=core[0][:], func=ACT.Square,
+                    scale=(-1.0, 1.0)[odd], bias=(1.0, 0.0)[odd],
+                )
+
             if kind == "silu":
-                return parts
-            r, sq = parts[:2]
-            bump = stage.tile([P, WORDS], BF16, tag="bump")
-            nc.vector.scalar_tensor_tensor(
-                out=bump[:], in0=r[:], scalar=2.0, in1=sq[:], op0=ALU.subtract, op1=ALU.mult
-            )
+                return [lambda: silu(0), lambda: silu(1)]
             if t == 0:
-                e, core_squares = parts[2:]
-                for odd, shift, half in ((0, 1.0, 0.5), (1, -2.0, -0.5)):
-                    core_sq = core_squares[odd]
-                    nc.vector.scalar_tensor_tensor(
-                        out=core_sq[:], in0=e[:], scalar=shift, in1=core_sq[:], op0=ALU.add, op1=ALU.mult
-                    )
-                    neg_k[odd] = core_pool.tile([P, WORDS], BF16, name="neg_k%d" % odd)
-                    nc.vector.tensor_scalar(
-                        out=neg_k[odd][:], in0=core_sq[:], scalar1=half, scalar2=2.0 / 3.0,
-                        op0=ALU.mult, op1=ALU.subtract,
-                    )
-            nc.vector.tensor_max(out=bump[:], in0=bump[:], in1=neg_k[t % 2][:])
-            nc.vector.tensor_scalar(
-                out=bump[:], in0=bump[:], scalar1=-1.0, scalar2=0.0, op0=ALU.mult, op1=ALU.max
-            )
-            left = stage.tile([P, WORDS], BF16, tag="left")
-            nc.vector.tensor_single_scalar(
-                out=left[:], in_=xT[:, g].rearrange("p b t -> p (b t)"), scalar=0.4 * t - 0.6, op=ALU.is_lt
-            )
-            acts = stage.tile([P, 2, WORDS], BF16, align_bytes=64, tag="acts")
-            nc.vector.tensor_mul(out=acts[:, 0, :], in0=bump[:], in1=left[:])
-            nc.vector.tensor_sub(out=acts[:, 1, :], in0=bump[:], in1=acts[:, 0, :])
-            return acts
+                return [
+                    fold, from_centre, from_even_bump, tail_square, from_odd_knot,
+                    lambda: core_square(0), lambda: core_square(1),
+                ]
+            return [fold, from_centre, tail_square]
 
+        def left_calls(step):
+            if step >= len(steps) or steps[step][0] == "silu":
+                return []
+            kind, g, t = steps[step]
 
-        def quantize_activations(step, acts):
+            def compare():
+                lefts[step] = left_pool.tile([P, WORDS], BF16, name="left")
+                nc.vector.tensor_single_scalar(
+                    out=lefts[step][:], in_=features(g), scalar=0.4 * t - 0.6, op=ALU.is_lt
+                )
+
+            return [compare]
+
+        def vector_calls(step):
+            kind, g, t = steps[step]
+            bump = {}
+
+            def cube():
+                bump[0] = stage.tile([P, WORDS], BF16, name="bump")
+                nc.vector.scalar_tensor_tensor(
+                    out=bump[0][:], in0=distance[step][:], scalar=2.0, in1=square[step][:],
+                    op0=ALU.subtract, op1=ALU.mult,
+                )
+
+            def core_cube(odd):
+                nc.vector.scalar_tensor_tensor(
+                    out=core[1 + odd][:], in0=core[0][:], scalar=(1.0, -2.0)[odd], in1=core[1 + odd][:],
+                    op0=ALU.add, op1=ALU.mult,
+                )
+
+            def core_value(odd):
+                neg_k[odd] = stage.tile([P, WORDS], BF16, name="neg_k%d" % odd)
+                nc.vector.tensor_scalar(
+                    out=neg_k[odd][:], in0=core[1 + odd][:], scalar1=(0.5, -0.5)[odd], scalar2=2.0 / 3.0,
+                    op0=ALU.mult, op1=ALU.subtract,
+                )
+
+            def core_or_tail():
+                nc.vector.tensor_max(out=bump[0][:], in0=bump[0][:], in1=neg_k[t % 2][:])
+
+            def positive_part():
+                nc.vector.tensor_scalar(
+                    out=bump[0][:], in0=bump[0][:], scalar1=-1.0, scalar2=0.0, op0=ALU.mult, op1=ALU.max
+                )
+
+            def left_basis():
+                acts[step] = stage.tile([P, 2, WORDS], BF16, align_bytes=64, name="acts")
+                nc.vector.tensor_mul(out=acts[step][:, 0, :], in0=bump[0][:], in1=lefts[step][:])
+
+            def right_basis():
+                nc.vector.tensor_sub(out=acts[step][:, 1, :], in0=bump[0][:], in1=acts[step][:, 0, :])
+
+            if kind == "silu":
+                return []
+            cores = [lambda: core_cube(0), lambda: core_cube(1), lambda: core_value(0), lambda: core_value(1)]
+            return [cube] + (cores if t == 0 else []) + [core_or_tail, positive_part, left_basis, right_basis]
+
+        def quantize_activations(step):
             nc.vector.quantize_mx(
                 out=a_codes[:, step].rearrange("p s b -> p (s b)").bitcast(FP8X4),
                 scales=a_scales[:, step].rearrange("p s b -> p (s b)"),
-                in_=acts[:].rearrange("p s w -> p (s w)"),
+                in_=acts[step][:].rearrange("p s w -> p (s w)"),
             )
 
         lstm_sb = keep.tile([P, B_TILES, U], BF16)
@@ -226,7 +318,6 @@ def tile_tkancell_pa_kernel(
         f_scales = keep.tile([P, 2, B], U8, align_bytes=64)
 
         def load_projection():
-            nc.sync.dma_start(out=lstm_sb[:], in_=lstm_out.rearrange("(n p) u -> p n u", p=P))
             nc.sync.dma_start(
                 out=c_raw[:].rearrange("p g t u -> p (g t) u"),
                 in_=combine_w.rearrange("(q p) u -> p q u", p=P),
@@ -234,14 +325,16 @@ def tile_tkancell_pa_kernel(
             nc.sync.dma_start(out=bias_sb[:], in_=combine_b.partition_broadcast(P))
 
         def transpose_lstm():
+            lt = acc_pool.tile([P, U_HALVES, B], BF16, name="acc_%d" % B_TILES)
             for n in range(B_TILES):
-                lt = small.tile([P, U_HALVES, P], BF16, tag="small")
                 for h in range(U_HALVES):
-                    nc.tensor.transpose(lt[:, h, :], lstm_sb[:, n, h * P : (h + 1) * P], ident[:])
-                copiers[n % 2](out=planes[:, 0, 0:U_HALVES, n * P : (n + 1) * P], in_=lt[:])
+                    nc.tensor.transpose(
+                        lt[:, h, n * P : (n + 1) * P], lstm_sb[:, n, h * P : (h + 1) * P], ident[:]
+                    )
+            nc.vector.tensor_copy(out=planes[:, 0, 0:U_HALVES, :], in_=lt[:])
 
         def quantize_projection():
-            c_grouped = grouped_pool.tile([P, 2, U, PACK], BF16, align_bytes=64, tag="w_grouped")
+            c_grouped = grouped_pool.tile([P, 2, U, PACK], BF16, align_bytes=64, name="w_grouped")
             for G in range(2):
                 copiers[G](
                     out=c_grouped[:, G].rearrange("p (c i) t -> p c t i", i=4),
@@ -259,7 +352,7 @@ def tile_tkancell_pa_kernel(
                 copiers[h](out=planes[:, plane // PACK, plane % PACK, :], in_=acc[(l, h)][:])
 
         def quantize_combined(G):
-            f_grouped = square_pool.tile([P, B, PACK], BF16, align_bytes=64, tag="sq")
+            f_grouped = square_pool.tile([P, B, PACK], BF16, align_bytes=64, name="sq")
             for i in range(2):
                 rows = slice(i * B // 2, (i + 1) * B // 2)
                 copiers[i](
@@ -276,45 +369,58 @@ def tile_tkancell_pa_kernel(
 
         for k in range(4):
             load(k)
+            if k == 0:
+                nc.sync.dma_start(out=lstm_sb[:], in_=lstm_out.rearrange("(n p) u -> p n u", p=P))
         for n in range(B_TILES):
             transpose_x(n)
-        parts = distances(0)
-        lay_out(0)
-        quantize_weights(0)
-        lay_out(1)
-        lay_out(2)
+        for k in range(3):
+            on_v, on_s = layout_calls(k)
+            weave(on_v, [])
+            if k == 0:
+                weave(scalar_calls(0), [])
+                weave(left_calls(0), [])
+            weave(on_s, [])
+            if k < 1:
+                transpose_lstm()
+                quantize_weights(k)
+        open_accumulators()
+        pending = []
         for k in range(len(units)):
             if k + 4 < len(units):
                 load(k + 4)
             if k == 0:
                 load_projection()
+            on_v, on_s = layout_calls(k + 3)
             step, l = units[k][0]
+            fill = [lambda step=s: quantize_activations(step) for s in pending] + on_v
+            if k > 0:
+                fill.append(lambda: quantize_weights(k))
+            pending = []
             if l == 0:
-                ahead = distances(step + 1) if step + 1 < len(steps) else None
-                quantize_activations(step, bases(step, parts))
-                parts = ahead
-            if k == 2:
-                transpose_lstm()
-            if k == 11:
-                quantize_projection()
-            if k + 3 < len(units):
-                lay_out(k + 3)
-            if k + 1 < len(units):
-                quantize_weights(k + 1)
-            multiply(k)
+                weave(scalar_calls(step + 1), on_s)
+                weave(vector_calls(step), fill + left_calls(step + 1))
+                pending = [step]
+            else:
+                weave(on_s, [])
+                weave(fill, [])
+            if k > 0:
+                multiply(k - 1)
             if k == len(units) - 3:
+                quantize_projection()
+            if k == len(units) - 2:
                 copy_out(0)
                 copy_out(1)
-            if k == len(units) - 2:
+            if k == len(units) - 1:
                 quantize_combined(0)
+        multiply(len(units) - 1)
         copy_out(L - 1)
         quantize_combined(1)
 
-        result = stage.tile([P, B_TILES, U], F32, align_bytes=64, tag="acts")
+        result = stage.tile([P, B_TILES, U], F32, align_bytes=64, name="acts")
         out_rows = out.rearrange("(n p) u -> p n u", p=P)
         for n in range(B_TILES):
             rows = slice(n * P, (n + 1) * P)
-            proj = small.tile([P, U], F32, tag="small")
+            proj = small.tile([P, U], F32, name="small")
             for G in range(2):
                 nc.tensor.matmul_mx(
                     out=proj[:],

@@ -41,7 +41,7 @@ def tile_tkancell_pa_kernel(
         keep = ctx.enter_context(tc.tile_pool(name="keep", bufs=1))
         raw_pool = ctx.enter_context(tc.tile_pool(name="raw", bufs=4))
         grouped_pool = ctx.enter_context(tc.tile_pool(name="grouped", bufs=4))
-        w_pool = ctx.enter_context(tc.tile_pool(name="w", bufs=2))
+        w_pool = ctx.enter_context(tc.tile_pool(name="w", bufs=3))
         stage = ctx.enter_context(tc.tile_pool(name="stage", bufs=1))
         left_pool = ctx.enter_context(tc.tile_pool(name="left", bufs=2))
         wide = ctx.enter_context(tc.tile_pool(name="wide", bufs=3))
@@ -136,16 +136,21 @@ def tile_tkancell_pa_kernel(
                 [lambda: lay_out(k, on_scalar, cut, half), lambda: lay_out(k, on_scalar, half, columns)],
             )
 
-        def quantize_weights(k):
-            w_codes = w_pool.tile([P, 4, U], U32, align_bytes=64, tag="w_codes")
-            w_scales = w_pool.tile([P, 4, U], U8, align_bytes=64, tag="w_scales")
-            passes = 2 * len(units[k])
+        def quantize_weights(k, i):
+            if k not in coded:
+                w_codes = w_pool.tile([P, 4, U], U32, align_bytes=64, tag="w_codes")
+                w_scales = w_pool.tile([P, 4, U], U8, align_bytes=64, tag="w_scales")
+                coded[k] = w_codes, w_scales
+            w_codes, w_scales = coded[k]
+            passes = slice(2 * i, 2 * i + 2)
             nc.vector.quantize_mx(
-                out=w_codes[:, :passes].rearrange("p q u -> p (q u)").bitcast(FP8X4),
-                scales=w_scales[:, :passes].rearrange("p q u -> p (q u)"),
-                in_=grouped[k][:, : passes * U].rearrange("p c t -> p (c t)"),
+                out=w_codes[:, passes].rearrange("p q u -> p (q u)").bitcast(FP8X4),
+                scales=w_scales[:, passes].rearrange("p q u -> p (q u)"),
+                in_=grouped[k][:, 2 * i * U : 2 * (i + 1) * U].rearrange("p c t -> p (c t)"),
             )
-            coded[k] = w_codes, w_scales
+
+        def quantize_calls(k):
+            return [lambda i=i: quantize_weights(k, i) for i in range(len(units[k]))]
 
         xT = keep.tile([P, D_HALVES, B, PACK], BF16)
         x_words = x_sb[:].bitcast(F32)
@@ -336,7 +341,7 @@ def tile_tkancell_pa_kernel(
         def quantize_projection():
             c_grouped = grouped_pool.tile([P, 2, U, PACK], BF16, align_bytes=64, name="w_grouped")
             for G in range(2):
-                copiers[G](
+                on_scalar(
                     out=c_grouped[:, G].rearrange("p (c i) t -> p c t i", i=4),
                     in_=c_raw[:, G].rearrange("p t (c i) -> p c t i", i=4),
                 )
@@ -346,16 +351,17 @@ def tile_tkancell_pa_kernel(
                 in_=c_grouped[:].rearrange("p g u t -> p (g u t)"),
             )
 
-        def copy_out(l):
+        def copy_out(l, engines):
             for h in range(U_HALVES):
                 plane = U_HALVES + l * U_HALVES + h
-                copiers[h](out=planes[:, plane // PACK, plane % PACK, :], in_=acc[(l, h)][:])
+                engines[h](out=planes[:, plane // PACK, plane % PACK, :], in_=acc[(l, h)][:])
 
-        def quantize_combined(G):
+        def quantize_combined(G, cut):
             f_grouped = square_pool.tile([P, B, PACK], BF16, align_bytes=64, name="sq")
-            for i in range(2):
-                rows = slice(i * B // 2, (i + 1) * B // 2)
-                copiers[i](
+            for copy, rows in ((on_vector, slice(0, cut)), (on_scalar, slice(cut, B))):
+                if rows.stop == rows.start:
+                    continue
+                copy(
                     out=f_grouped[:, rows].rearrange("p (c i) t -> p c t i", i=4),
                     in_=planes[:, G, :, rows].rearrange("p t (c i) -> p c t i", i=4),
                 )
@@ -365,6 +371,24 @@ def tile_tkancell_pa_kernel(
                     out=f_codes[:, G, rows].bitcast(FP8X4),
                     scales=f_scales[:, G, rows],
                     in_=f_grouped[:, rows].rearrange("p b t -> p (b t)"),
+                )
+
+        proj = []
+
+        def project(G):
+            for n in range(B_TILES):
+                if G == 0:
+                    bank = acc_pool.tile([P, U], F32, name="acc_%d" % n)
+                    proj.append(bank)
+                rows = slice(n * P, (n + 1) * P)
+                nc.tensor.matmul_mx(
+                    out=proj[n][:],
+                    lhsT=f_codes[:, G, rows].bitcast(FP8X4),
+                    lhsT_scale=f_scales[:, G, rows],
+                    rhs=c_codes[:, G, :].bitcast(FP8X4),
+                    rhs_scale=c_scales[:, G, :],
+                    start=(G == 0),
+                    stop=(G == 1),
                 )
 
         for k in range(4):
@@ -382,7 +406,7 @@ def tile_tkancell_pa_kernel(
             weave(on_s, [])
             if k < 1:
                 transpose_lstm()
-                quantize_weights(k)
+                weave(quantize_calls(k), [])
         open_accumulators()
         pending = []
         for k in range(len(units)):
@@ -393,12 +417,13 @@ def tile_tkancell_pa_kernel(
             on_v, on_s = layout_calls(k + 3)
             step, l = units[k][0]
             fill = [lambda step=s: quantize_activations(step) for s in pending] + on_v
+            fill += left_calls(step + 1) if l == 0 else []
             if k > 0:
-                fill.append(lambda: quantize_weights(k))
+                fill += quantize_calls(k)
             pending = []
             if l == 0:
                 weave(scalar_calls(step + 1), on_s)
-                weave(vector_calls(step), fill + left_calls(step + 1))
+                weave(vector_calls(step), fill)
                 pending = [step]
             else:
                 weave(on_s, [])
@@ -408,28 +433,18 @@ def tile_tkancell_pa_kernel(
             if k == len(units) - 3:
                 quantize_projection()
             if k == len(units) - 2:
-                copy_out(0)
-                copy_out(1)
+                copy_out(0, copiers)
+                copy_out(1, copiers)
             if k == len(units) - 1:
-                quantize_combined(0)
+                quantize_combined(0, 256)
+        project(0)
         multiply(len(units) - 1)
-        copy_out(L - 1)
-        quantize_combined(1)
+        copy_out(L - 1, copiers)
+        quantize_combined(1, 320)
 
+        project(1)
         result = stage.tile([P, B_TILES, U], F32, align_bytes=64, name="acts")
         out_rows = out.rearrange("(n p) u -> p n u", p=P)
         for n in range(B_TILES):
-            rows = slice(n * P, (n + 1) * P)
-            proj = small.tile([P, U], F32, name="small")
-            for G in range(2):
-                nc.tensor.matmul_mx(
-                    out=proj[:],
-                    lhsT=f_codes[:, G, rows].bitcast(FP8X4),
-                    lhsT_scale=f_scales[:, G, rows],
-                    rhs=c_codes[:, G, :].bitcast(FP8X4),
-                    rhs_scale=c_scales[:, G, :],
-                    start=(G == 0),
-                    stop=(G == 1),
-                )
-            nc.vector.tensor_add(out=result[:, n, :], in0=proj[:], in1=bias_sb[:])
+            nc.vector.tensor_add(out=result[:, n, :], in0=proj[n][:], in1=bias_sb[:])
             nc.sync.dma_start(out=out_rows[:, n, :], in_=result[:, n, :])

@@ -71,7 +71,7 @@ def tile_tkancell_pa_kernel(
 
         units = [[(step, 0), (step, 1)] for step in range(len(steps))]
         thirds = [[(step, 2) for step in range(first, min(first + 2, len(steps)))] for first in range(0, len(steps), 2)]
-        units = units[:8] + thirds[:1] + units[8:] + thirds[1:]
+        units = units[:8] + thirds[:2] + units[8:] + thirds[2:]
 
         base_rows = kan_base_w.rearrange("l (g p t) u -> l g p t u", g=D_HALVES, t=PACK, p=P)
         spline_rows = kan_spline_w.rearrange(
@@ -99,7 +99,7 @@ def tile_tkancell_pa_kernel(
                 in_=rows[:, :, first:last].rearrange("p t (c i) -> p c t i", i=4),
             )
 
-        moves = [(k, q) for k in range(4, 9) for q in range(2 * len(units[k]))]
+        moves = [(k, q) for k in range(5, 10) for q in range(2 * len(units[k]))]
         moved = {}
 
         def move(i):
@@ -127,9 +127,9 @@ def tile_tkancell_pa_kernel(
             if k >= len(units):
                 return [], []
             columns = 2 * U * len(units[k])
-            if 4 <= k < 9:
+            if 5 <= k < 10:
                 return [], [lambda q=q: copy_moved(k, q) for q in range(2 * len(units[k]))]
-            cut = min(1024 if k < 4 else 0, columns)
+            cut = min(1024 if k < 5 else 0, columns)
             half = (cut + columns) // 32 * 16
             return (
                 [lambda: lay_out(k, on_vector, 0, cut)],
@@ -237,7 +237,7 @@ def tile_tkancell_pa_kernel(
                 core[1 + odd] = square_pool.tile([P, WORDS], F32, align_bytes=64, name="sq")
                 nc.scalar.activation(
                     out=core[1 + odd][:], in_=core[0][:], func=ACT.Square,
-                    scale=(-1.0, 1.0)[odd], bias=(1.0, 0.0)[odd],
+                    scale=(-1.0, 1.0)[odd] * math.sqrt(0.5), bias=(1.0, -0.5)[odd] * math.sqrt(0.5),
                 )
 
             if kind == "silu":
@@ -273,17 +273,22 @@ def tile_tkancell_pa_kernel(
                     op0=ALU.subtract, op1=ALU.mult,
                 )
 
-            def core_cube(odd):
+            def core_cube():
                 nc.vector.scalar_tensor_tensor(
-                    out=core[1 + odd][:], in0=core[0][:], scalar=(1.0, -2.0)[odd], in1=core[1 + odd][:],
-                    op0=ALU.add, op1=ALU.mult,
+                    out=core[1][:], in0=core[0][:], scalar=1.0, in1=core[1][:], op0=ALU.add, op1=ALU.mult,
                 )
 
-            def core_value(odd):
-                neg_k[odd] = stage.tile([P, WORDS], BF16, name="neg_k%d" % odd)
-                nc.vector.tensor_scalar(
-                    out=neg_k[odd][:], in0=core[1 + odd][:], scalar1=(0.5, -0.5)[odd], scalar2=2.0 / 3.0,
-                    op0=ALU.mult, op1=ALU.subtract,
+            def even_core():
+                neg_k[0] = stage.tile([P, WORDS], BF16, name="neg_k0")
+                nc.vector.tensor_single_scalar(
+                    out=neg_k[0][:], in_=core[1][:], scalar=2.0 / 3.0, op=ALU.subtract
+                )
+
+            def odd_core():
+                neg_k[1] = stage.tile([P, WORDS], BF16, name="neg_k1")
+                nc.vector.scalar_tensor_tensor(
+                    out=neg_k[1][:], in0=core[2][:], scalar=7.0 / 24.0, in1=core[1][:],
+                    op0=ALU.subtract, op1=ALU.subtract,
                 )
 
             def core_or_tail():
@@ -303,7 +308,7 @@ def tile_tkancell_pa_kernel(
 
             if kind == "silu":
                 return []
-            cores = [lambda: core_cube(0), lambda: core_cube(1), lambda: core_value(0), lambda: core_value(1)]
+            cores = [core_cube, even_core, odd_core]
             return [cube] + (cores if t == 0 else []) + [core_or_tail, positive_part, left_basis, right_basis]
 
         def quantize_activations(step):

@@ -99,7 +99,7 @@ def tile_tkancell_pa_kernel(
                 in_=rows[:, :, first:last].rearrange("p t (c i) -> p c t i", i=4),
             )
 
-        moves = [(k, q) for k in range(5, 10) for q in range(2 * len(units[k]))]
+        moves = [(k, q) for k in range(5, len(units)) for q in range(2 * len(units[k]))][:22]
         moved = {}
 
         def move(i):
@@ -127,13 +127,15 @@ def tile_tkancell_pa_kernel(
             if k >= len(units):
                 return [], []
             columns = 2 * U * len(units[k])
-            if 5 <= k < 10:
-                return [], [lambda q=q: copy_moved(k, q) for q in range(2 * len(units[k]))]
             cut = min(1024 if k < 5 else 0, columns)
-            half = (cut + columns) // 32 * 16
+            banks = [q for q in range(2 * len(units[k])) if (k, q) in moves]
+            start = cut + len(banks) * U
+            half = (start + columns) // 32 * 16
+            piece = U if k == 0 else 4 * U
             return (
-                [lambda: lay_out(k, on_vector, 0, cut)],
-                [lambda: lay_out(k, on_scalar, cut, half), lambda: lay_out(k, on_scalar, half, columns)],
+                [lambda i=i: lay_out(k, on_vector, i, min(i + piece, cut)) for i in range(0, cut, piece)],
+                [lambda q=q: copy_moved(k, q) for q in banks]
+                + [lambda: lay_out(k, on_scalar, start, half), lambda: lay_out(k, on_scalar, half, columns)],
             )
 
         def quantize_weights(k, i):
@@ -208,9 +210,11 @@ def tile_tkancell_pa_kernel(
 
             def fold():
                 distance[step] = wide.tile([P, WORDS], F32, name="dist")
-                nc.scalar.activation(
-                    out=distance[step][:], in_=features(g), func=ACT.Abs, scale=2.5, bias=1.5 - t
-                )
+                half = WORDS // 2
+                for span in [slice(0, half), slice(half, WORDS)] if step == 0 else [slice(0, WORDS)]:
+                    nc.scalar.activation(
+                        out=distance[step][:, span], in_=features(g)[:, span], func=ACT.Abs, scale=2.5, bias=1.5 - t
+                    )
 
             def from_centre():
                 nc.scalar.activation(
@@ -237,7 +241,7 @@ def tile_tkancell_pa_kernel(
                 core[1 + odd] = square_pool.tile([P, WORDS], F32, align_bytes=64, name="sq")
                 nc.scalar.activation(
                     out=core[1 + odd][:], in_=core[0][:], func=ACT.Square,
-                    scale=(-1.0, 1.0)[odd] * math.sqrt(0.5), bias=(1.0, -0.5)[odd] * math.sqrt(0.5),
+                    scale=math.sqrt(0.5), bias=(0.0, -0.5)[odd] * math.sqrt(0.5),
                 )
 
             if kind == "silu":
@@ -275,20 +279,20 @@ def tile_tkancell_pa_kernel(
 
             def core_cube():
                 nc.vector.scalar_tensor_tensor(
-                    out=core[1][:], in0=core[0][:], scalar=1.0, in1=core[1][:], op0=ALU.add, op1=ALU.mult,
-                )
-
-            def even_core():
-                neg_k[0] = stage.tile([P, WORDS], BF16, name="neg_k0")
-                nc.vector.tensor_single_scalar(
-                    out=neg_k[0][:], in_=core[1][:], scalar=2.0 / 3.0, op=ALU.subtract
+                    out=core[1][:], in0=core[0][:], scalar=2.0, in1=core[1][:], op0=ALU.subtract, op1=ALU.mult,
                 )
 
             def odd_core():
                 neg_k[1] = stage.tile([P, WORDS], BF16, name="neg_k1")
+                nc.vector.tensor_scalar(
+                    out=neg_k[1][:], in0=core[1][:], scalar1=-1.0, scalar2=2.0 / 3.0, op0=ALU.mult, op1=ALU.subtract
+                )
+
+            def even_core():
+                neg_k[0] = stage.tile([P, WORDS], BF16, name="neg_k0")
                 nc.vector.scalar_tensor_tensor(
-                    out=neg_k[1][:], in0=core[2][:], scalar=7.0 / 24.0, in1=core[1][:],
-                    op0=ALU.subtract, op1=ALU.subtract,
+                    out=neg_k[0][:], in0=core[2][:], scalar=7.0 / 24.0, in1=core[1][:],
+                    op0=ALU.subtract, op1=ALU.add,
                 )
 
             def core_or_tail():
@@ -308,7 +312,7 @@ def tile_tkancell_pa_kernel(
 
             if kind == "silu":
                 return []
-            cores = [core_cube, even_core, odd_core]
+            cores = [core_cube, odd_core, even_core]
             return [cube] + (cores if t == 0 else []) + [core_or_tail, positive_part, left_basis, right_basis]
 
         def quantize_activations(step):
@@ -400,11 +404,12 @@ def tile_tkancell_pa_kernel(
             load(k)
             if k == 0:
                 nc.sync.dma_start(out=lstm_sb[:], in_=lstm_out.rearrange("(n p) u -> p n u", p=P))
-        for n in range(B_TILES):
-            transpose_x(n)
+        on_v, on_s = layout_calls(0)
+        weave([lambda n=n: transpose_x(n) for n in range(B_TILES)], on_v)
         for k in range(3):
             on_v, on_s = layout_calls(k)
-            weave(on_v, [])
+            if k > 0:
+                weave(on_v, [])
             if k == 0:
                 weave(scalar_calls(0), [])
                 weave(left_calls(0), [])

@@ -59,10 +59,18 @@ def tile_tkancell_pa_kernel(
         make_identity(nc, ident_words[:])
         ctx.enter_context(tc.manual_schedule())
 
-        x_sb = square_pool.tile([P, B_TILES, D], BF16, align_bytes=64, name="sq")
+        x_halves = []
         x_rows = x.rearrange("(n p) d -> p n d", p=P)
-        for n in range(B_TILES):
-            nc.sync.dma_start(out=x_sb[:, n, :], in_=x_rows[:, n, :])
+
+        def load_x(g):
+            x_half = square_pool.tile([P, B_TILES, K_PASS], BF16, align_bytes=64, name="sq")
+            for n in range(0, B_TILES, 2):
+                tiles = slice(n, n + 2)
+                nc.sync.dma_start(
+                    out=x_half[:, tiles, :], in_=x_rows[:, tiles, g * K_PASS : (g + 1) * K_PASS]
+                )
+            x_halves.append(x_half)
+
 
         steps = [("basis", g, t) for g in range(D_HALVES) for t in range(FOLD)]
         steps.insert(1, ("silu", 0, 0))
@@ -155,19 +163,17 @@ def tile_tkancell_pa_kernel(
             return [lambda i=i: quantize_weights(k, i) for i in range(len(units[k]))]
 
         xT = keep.tile([P, D_HALVES, B, PACK], BF16)
-        x_words = x_sb[:].bitcast(F32)
         xT_words = xT[:].bitcast(F32)
 
-        def transpose_x(n):
-            xt = acc_pool.tile([P, D_HALVES, 2, P], F32, name="acc_%d" % n)
-            for g in range(D_HALVES):
+        def transpose_x(g, m):
+            xt = acc_pool.tile([P, 2, 2, P], F32, name="acc_%d" % (2 * g + m))
+            for i in range(2):
+                words = x_halves[g][:].bitcast(F32)[:, 2 * m + i, :]
                 for u in range(2):
-                    first = g * (K_PASS // 2) + u
-                    nc.tensor.transpose(
-                        xt[:, g, u, :], x_words[:, n, first : (g + 1) * (K_PASS // 2) : 2], ident_words[:]
-                    )
-            copiers[n % 2](
-                out=xT_words[:, :, n * P : (n + 1) * P, :], in_=xt[:].rearrange("p g u r -> p g r u")
+                    nc.tensor.transpose(xt[:, i, u, :], words[:, u : K_PASS // 2 : 2], ident_words[:])
+            copiers[m](
+                out=xT_words[:, g, 2 * m * P : 2 * (m + 1) * P, :].rearrange("p (i r) u -> p i r u", i=2),
+                in_=xt[:].rearrange("p i u r -> p i r u"),
             )
 
         acc = {}
@@ -400,12 +406,16 @@ def tile_tkancell_pa_kernel(
                     stop=(G == 1),
                 )
 
+        load_x(0)
         for k in range(4):
             load(k)
             if k == 0:
+                load_x(1)
                 nc.sync.dma_start(out=lstm_sb[:], in_=lstm_out.rearrange("(n p) u -> p n u", p=P))
         on_v, on_s = layout_calls(0)
-        weave([lambda n=n: transpose_x(n) for n in range(B_TILES)], on_v)
+        transpose_x(0, 0)
+        transpose_x(0, 1)
+        weave(on_v, [])
         for k in range(3):
             on_v, on_s = layout_calls(k)
             if k > 0:
@@ -413,11 +423,14 @@ def tile_tkancell_pa_kernel(
             if k == 0:
                 weave(scalar_calls(0), [])
                 weave(left_calls(0), [])
+                transpose_x(1, 0)
+                transpose_x(1, 1)
             weave(on_s, [])
             if k < 1:
                 transpose_lstm()
                 weave(quantize_calls(k), [])
         open_accumulators()
+        last_shared = units.index([(len(steps) - 1, 0), (len(steps) - 1, 1)])
         pending = []
         for k in range(len(units)):
             if k + 4 < len(units):
@@ -442,10 +455,10 @@ def tile_tkancell_pa_kernel(
                 multiply(k - 1)
             if k == len(units) - 3:
                 quantize_projection()
-            if k == len(units) - 2:
+            if k == last_shared + 1:
                 copy_out(0, copiers)
                 copy_out(1, copiers)
-            if k == len(units) - 1:
+            if k == min(last_shared + 2, len(units) - 1):
                 quantize_combined(0, 256)
         project(0)
         multiply(len(units) - 1)

@@ -123,9 +123,6 @@ def tile_tkancell_pa_kernel(
 
         def copy_moved(k, q):
             i = moves.index((k, q))
-            if i == 0:
-                move(0)
-                move(1)
             if k not in grouped:
                 grouped[k] = grouped_pool.tile([P, 4 * U, PACK], BF16, align_bytes=64, name="w_grouped")
             on_scalar(out=grouped[k][:, q * U : (q + 1) * U, :], in_=moved[i][:])
@@ -139,7 +136,7 @@ def tile_tkancell_pa_kernel(
             banks = [q for q in range(2 * len(units[k])) if (k, q) in moves]
             start = cut + len(banks) * U
             half = (start + columns) // 32 * 16
-            piece = U if k == 0 else 4 * U
+            piece = U if k in (0, 4) else 4 * U
             return (
                 [lambda i=i: lay_out(k, on_vector, i, min(i + piece, cut)) for i in range(0, cut, piece)],
                 [lambda q=q: copy_moved(k, q) for q in banks]
@@ -318,14 +315,12 @@ def tile_tkancell_pa_kernel(
 
             if kind == "silu":
                 return []
-            cores = [core_cube, odd_core, even_core]
+            cores = [lambda: (core_cube(), odd_core(), even_core())]
             return [cube] + (cores if t == 0 else []) + [core_or_tail, positive_part, left_basis, right_basis]
 
-        def quantize_activations(step):
+        def quantize_activations(step, s):
             nc.vector.quantize_mx(
-                out=a_codes[:, step].rearrange("p s b -> p (s b)").bitcast(FP8X4),
-                scales=a_scales[:, step].rearrange("p s b -> p (s b)"),
-                in_=acts[step][:].rearrange("p s w -> p (s w)"),
+                out=a_codes[:, step, s, :].bitcast(FP8X4), scales=a_scales[:, step, s, :], in_=acts[step][:, s, :]
             )
 
         lstm_sb = keep.tile([P, B_TILES, U], BF16)
@@ -338,6 +333,7 @@ def tile_tkancell_pa_kernel(
         f_scales = keep.tile([P, 2, B], U8, align_bytes=64)
 
         def load_projection():
+            nc.sync.dma_start(out=lstm_sb[:], in_=lstm_out.rearrange("(n p) u -> p n u", p=P))
             nc.sync.dma_start(
                 out=c_raw[:].rearrange("p g t u -> p (g t) u"),
                 in_=combine_w.rearrange("(q p) u -> p q u", p=P),
@@ -345,13 +341,13 @@ def tile_tkancell_pa_kernel(
             nc.sync.dma_start(out=bias_sb[:], in_=combine_b.partition_broadcast(P))
 
         def transpose_lstm():
-            lt = acc_pool.tile([P, U_HALVES, B], BF16, name="acc_%d" % B_TILES)
+            lt = small.tile([P, U_HALVES, B], BF16, name="small")
             for n in range(B_TILES):
                 for h in range(U_HALVES):
                     nc.tensor.transpose(
                         lt[:, h, n * P : (n + 1) * P], lstm_sb[:, n, h * P : (h + 1) * P], ident[:]
                     )
-            nc.vector.tensor_copy(out=planes[:, 0, 0:U_HALVES, :], in_=lt[:])
+            nc.scalar.copy(out=planes[:, 0, 0:U_HALVES, :], in_=lt[:])
 
         def quantize_projection():
             c_grouped = grouped_pool.tile([P, 2, U, PACK], BF16, align_bytes=64, name="w_grouped")
@@ -411,7 +407,6 @@ def tile_tkancell_pa_kernel(
             load(k)
             if k == 0:
                 load_x(1)
-                nc.sync.dma_start(out=lstm_sb[:], in_=lstm_out.rearrange("(n p) u -> p n u", p=P))
         on_v, on_s = layout_calls(0)
         transpose_x(0, 0)
         transpose_x(0, 1)
@@ -426,22 +421,25 @@ def tile_tkancell_pa_kernel(
                 transpose_x(1, 0)
                 transpose_x(1, 1)
             weave(on_s, [])
-            if k < 1:
-                transpose_lstm()
-                weave(quantize_calls(k), [])
+            weave(quantize_calls(k), [])
         open_accumulators()
         last_shared = units.index([(len(steps) - 1, 0), (len(steps) - 1, 1)])
         pending = []
         for k in range(len(units)):
             if k + 4 < len(units):
                 load(k + 4)
-            if k == 0:
+            if k == 4:
                 load_projection()
             on_v, on_s = layout_calls(k + 3)
+            if k == 0:
+                on_v += layout_calls(4)[0]
+            if k == 1:
+                on_v = []
             step, l = units[k][0]
-            fill = [lambda step=s: quantize_activations(step) for s in pending] + on_v
+            fill = [lambda made=made, s=s: quantize_activations(made, s) for made in pending for s in range(2)]
+            fill += on_v
             fill += left_calls(step + 1) if l == 0 else []
-            if k > 0:
+            if k >= 3:
                 fill += quantize_calls(k)
             pending = []
             if l == 0:
@@ -451,10 +449,15 @@ def tile_tkancell_pa_kernel(
             else:
                 weave(on_s, [])
                 weave(fill, [])
+            if k == 1:
+                move(0)
+                move(1)
             if k > 0:
                 multiply(k - 1)
             if k == len(units) - 3:
                 quantize_projection()
+            if k == 7:
+                transpose_lstm()
             if k == last_shared + 1:
                 copy_out(0, copiers)
                 copy_out(1, copiers)

@@ -21,6 +21,7 @@ FOLD = NB // 2
 D_HALVES = D // K_PASS
 B_TILES = B // P
 U_HALVES = U // P
+ROWS = B // 2
 WORDS = B * PACK
 
 FLOPS = 2 * B * (D + D * NB) * L * U + 2 * B * (1 + L) * U * U
@@ -176,25 +177,36 @@ def tile_tkancell_pa_kernel(
         acc = {}
 
         def open_accumulators():
-            for l in range(L):
+            for l in range(L - 1):
                 for h in range(U_HALVES):
                     acc[(l, h)] = acc_pool.tile([P, B], F32, name="acc_%d" % (U_HALVES * l + h))
 
-        def multiply(k):
+        def open_last_accumulators():
+            for h in range(U_HALVES):
+                acc[(L - 1, h, 0)] = acc_pool.tile([P, ROWS], F32, name="acc_%d" % (B_TILES + h))
+                acc[(L - 1, h, 1)] = small.tile([P, ROWS], F32, name="small")
+
+        def multiply(k, halves=(0, 1)):
             w_codes, w_scales = coded[k]
             for i, (step, l) in enumerate(units[k]):
-                for s in range(2):
-                    for h in range(U_HALVES):
-                        cols = slice(h * P, (h + 1) * P)
-                        nc.tensor.matmul_mx(
-                            out=acc[(l, h)][:],
-                            lhsT=w_codes[:, 2 * i + s, cols].bitcast(FP8X4),
-                            lhsT_scale=w_scales[:, 2 * i + s, cols],
-                            rhs=a_codes[:, step, s, :].bitcast(FP8X4),
-                            rhs_scale=a_scales[:, step, s, :],
-                            start=(step == 0 and s == 0),
-                            stop=(step == len(steps) - 1 and s == 1),
-                        )
+                if l == L - 1 and (l, 0, 0) not in acc:
+                    open_last_accumulators()
+                pieces = [(i, half) for half in halves] if l == L - 1 else [(i, None)]
+                for i, half in pieces:
+                    rows = slice(0, B) if half is None else slice(half * ROWS, (half + 1) * ROWS)
+                    for s in range(2):
+                        for h in range(U_HALVES):
+                            cols = slice(h * P, (h + 1) * P)
+                            out_sums = acc[(l, h)] if half is None else acc[(l, h, half)]
+                            nc.tensor.matmul_mx(
+                                out=out_sums[:],
+                                lhsT=w_codes[:, 2 * i + s, cols].bitcast(FP8X4),
+                                lhsT_scale=w_scales[:, 2 * i + s, cols],
+                                rhs=a_codes[:, step, s, rows].bitcast(FP8X4),
+                                rhs_scale=a_scales[:, step, s, rows],
+                                start=(step == 0 and s == 0),
+                                stop=(step == len(steps) - 1 and s == 1),
+                            )
 
         acts, lefts, distance, square, core, neg_k = {}, {}, {}, {}, {}, {}
 
@@ -367,27 +379,37 @@ def tile_tkancell_pa_kernel(
                 plane = U_HALVES + l * U_HALVES + h
                 engines[h](out=planes[:, plane // PACK, plane % PACK, :], in_=acc[(l, h)][:])
 
-        def quantize_combined(G, cut):
-            f_grouped = square_pool.tile([P, B, PACK], BF16, align_bytes=64, name="sq")
-            for copy, rows in ((on_vector, slice(0, cut)), (on_scalar, slice(cut, B))):
-                if rows.stop == rows.start:
-                    continue
+        def copy_out_rows(half):
+            rows = slice(half * ROWS, (half + 1) * ROWS)
+            for h in range(U_HALVES):
+                copiers[h](out=planes[:, 1, U_HALVES + h, rows], in_=acc[(L - 1, h, half)][:])
+
+        f_grouped = {}
+
+        def lay_out_combined(G, half, cut):
+            if G not in f_grouped:
+                f_grouped[G] = square_pool.tile([P, B, PACK], BF16, align_bytes=64, name="sq")
+            first = half * ROWS
+            for copy, rows in (
+                (on_vector, slice(first, first + cut)), (on_scalar, slice(first + cut, first + ROWS))
+            ):
                 copy(
-                    out=f_grouped[:, rows].rearrange("p (c i) t -> p c t i", i=4),
+                    out=f_grouped[G][:, rows].rearrange("p (c i) t -> p c t i", i=4),
                     in_=planes[:, G, :, rows].rearrange("p t (c i) -> p c t i", i=4),
                 )
-            for i in range(2):
-                rows = slice(i * B // 2, (i + 1) * B // 2)
-                nc.vector.quantize_mx(
-                    out=f_codes[:, G, rows].bitcast(FP8X4),
-                    scales=f_scales[:, G, rows],
-                    in_=f_grouped[:, rows].rearrange("p b t -> p (b t)"),
-                )
+
+        def quantize_combined(G, half):
+            rows = slice(half * ROWS, (half + 1) * ROWS)
+            nc.vector.quantize_mx(
+                out=f_codes[:, G, rows].bitcast(FP8X4),
+                scales=f_scales[:, G, rows],
+                in_=f_grouped[G][:, rows].rearrange("p b t -> p (b t)"),
+            )
 
         proj = []
 
-        def project(G):
-            for n in range(B_TILES):
+        def project(G, tiles):
+            for n in tiles:
                 if G == 0:
                     bank = acc_pool.tile([P, U], F32, name="acc_%d" % n)
                     proj.append(bank)
@@ -452,23 +474,33 @@ def tile_tkancell_pa_kernel(
             if k == 1:
                 move(0)
                 move(1)
-            if k > 0:
+            if k == len(units) - 1:
+                multiply(k - 1, [0])
+            elif k > 0:
                 multiply(k - 1)
             if k == len(units) - 3:
                 quantize_projection()
             if k == 7:
                 transpose_lstm()
             if k == last_shared + 1:
-                copy_out(0, copiers)
-                copy_out(1, copiers)
-            if k == min(last_shared + 2, len(units) - 1):
-                quantize_combined(0, 256)
-        project(0)
-        multiply(len(units) - 1)
-        copy_out(L - 1, copiers)
-        quantize_combined(1, 320)
+                copy_out(0, [on_scalar, on_scalar])
+                copy_out(1, [on_scalar, on_scalar])
+            if k == len(units) - 1:
+                for half in range(2):
+                    lay_out_combined(0, half, ROWS // 2)
+                for half in range(2):
+                    quantize_combined(0, half)
+        last = len(units) - 1
+        multiply(last, [0])
+        project(0, range(B_TILES))
+        multiply(last - 1, [1])
+        multiply(last, [1])
+        for half in range(2):
+            copy_out_rows(half)
+            lay_out_combined(1, half, 176)
+            quantize_combined(1, half)
+        project(1, range(B_TILES))
 
-        project(1)
         result = stage.tile([P, B_TILES, U], F32, align_bytes=64, name="acts")
         out_rows = out.rearrange("(n p) u -> p n u", p=P)
         for n in range(B_TILES):

@@ -104,8 +104,8 @@ def tile_tkancell_pa_kernel(
                 grouped[k] = grouped_pool.tile([P, 4 * U, PACK], BF16, align_bytes=64, name="w_grouped")
             rows = raws[k][:].rearrange("p t q u -> p t (q u)")
             copy(
-                out=grouped[k][:, first:last, :].rearrange("p (c i) t -> p c t i", i=4),
-                in_=rows[:, :, first:last].rearrange("p t (c i) -> p c t i", i=4),
+                out=grouped[k][:, first:last, :].rearrange("p (c i) t -> p c t i", i=8),
+                in_=rows[:, :, first:last].rearrange("p t (c i) -> p c t i", i=8),
             )
 
         moves = [(k, q) for k in range(5, len(units)) for q in range(2 * len(units[k]))][:22]

@@ -42,7 +42,7 @@ def tile_tkancell_pa_kernel(
         keep = ctx.enter_context(tc.tile_pool(name="keep", bufs=1))
         raw_pool = ctx.enter_context(tc.tile_pool(name="raw", bufs=4))
         grouped_pool = ctx.enter_context(tc.tile_pool(name="grouped", bufs=4))
-        w_pool = ctx.enter_context(tc.tile_pool(name="w", bufs=3))
+        w_pool = ctx.enter_context(tc.tile_pool(name="w", bufs=4))
         stage = ctx.enter_context(tc.tile_pool(name="stage", bufs=1))
         left_pool = ctx.enter_context(tc.tile_pool(name="left", bufs=2))
         wide = ctx.enter_context(tc.tile_pool(name="wide", bufs=3))
@@ -78,37 +78,58 @@ def tile_tkancell_pa_kernel(
         a_codes = keep.tile([P, len(steps), 2, B], U32, align_bytes=64)
         a_scales = keep.tile([P, len(steps), 2, B], U8, align_bytes=64)
 
-        units = [[(step, 0), (step, 1)] for step in range(len(steps))]
-        thirds = [[(step, 2) for step in range(first, min(first + 2, len(steps)))] for first in range(0, len(steps), 2)]
-        units = units[:8] + thirds[:2] + units[8:] + thirds[2:]
+        index = {step: i for i, step in enumerate(steps)}
+        silu = index[("silu", 0, 0)]
+        pairs = [(index[("basis", g, t)], index[("basis", g, t + 1)]) for g in range(D_HALVES) for t in range(0, FOLD, 2)]
+        units = [(pair, (l,)) for pair in pairs for l in range(L - 1)]
+        units.insert(2, ((silu,), (0, 1)))
+        thirds = [(pair, (L - 1,)) for pair in pairs] + [((silu,), (L - 1,))]
+        units = units[:8] + thirds[:1] + units[8:] + thirds[1:]
+        turn = {step: step if step < 8 else 9 for step in range(len(steps))}
+        made_at = {k: step for step, k in turn.items()}
+
+        def blocks(k):
+            unit_steps, layers = units[k]
+            return 2 if len(unit_steps) == 2 else len(layers)
 
         base_rows = kan_base_w.rearrange("l (g p t) u -> l g p t u", g=D_HALVES, t=PACK, p=P)
         spline_rows = kan_spline_w.rearrange(
-            "l (g p t k) u -> l g k p t u", g=D_HALVES, t=PACK, p=P, k=NB
+            "l (g p t h i k) u -> l g h i p t (k u)", g=D_HALVES, t=PACK, p=P, h=2, i=FOLD // 2, k=2
         )
         raws, grouped, coded = {}, {}, {}
 
         def load(k):
-            raw = raw_pool.tile([P, PACK, 4, U], BF16, tag="raw")
-            for i, (step, l) in enumerate(units[k]):
-                kind, g, t = steps[step]
+            raw = raw_pool.tile([P, 2, PACK, 2 * U], BF16, tag="raw")
+            unit_steps, layers = units[k]
+            if len(unit_steps) == 2:
+                kind, g, t = steps[unit_steps[0]]
                 for s in range(2):
-                    rows = base_rows[l, s] if kind == "silu" else spline_rows[l, g, t + s * FOLD]
-                    nc.sync.dma_start(out=raw[:, :, 2 * i + s, :], in_=rows)
+                    nc.sync.dma_start(out=raw[:, s], in_=spline_rows[layers[0], g, s, t // 2])
+            else:
+                for j, l in enumerate(layers):
+                    for s in range(2):
+                        nc.sync.dma_start(out=raw[:, j, :, s * U : (s + 1) * U], in_=base_rows[l, s])
             raws[k] = raw
+
+        def place(k, step, l, s):
+            unit_steps, layers = units[k]
+            if len(unit_steps) == 2:
+                return 2 * s + unit_steps.index(step)
+            return 2 * layers.index(l) + s
 
         def lay_out(k, copy, first, last):
             if last <= first:
                 return
             if k not in grouped:
                 grouped[k] = grouped_pool.tile([P, 4 * U, PACK], BF16, align_bytes=64, name="w_grouped")
-            rows = raws[k][:].rearrange("p t q u -> p t (q u)")
+            j = first // (2 * U)
+            columns = slice(first - 2 * j * U, last - 2 * j * U)
             copy(
                 out=grouped[k][:, first:last, :].rearrange("p (c i) t -> p c t i", i=8),
-                in_=rows[:, :, first:last].rearrange("p t (c i) -> p c t i", i=8),
+                in_=raws[k][:, j, :, columns].rearrange("p t (c i) -> p c t i", i=8),
             )
 
-        moves = [(k, q) for k in range(5, len(units)) for q in range(2 * len(units[k]))][:22]
+        moves = [(k, q) for k in range(5, len(units)) for q in range(2 * blocks(k))][2 : 2 + 22]
         moved = {}
 
         def move(i):
@@ -119,7 +140,7 @@ def tile_tkancell_pa_kernel(
             for t in range(0, PACK, 2):
                 nc.tensor.matmul(
                     moved[i][:, :, t : t + 2].rearrange("p c t -> p t c"),
-                    lhsT=ident[:], rhs=raws[k][:, t : t + 2, q, :], start=True, stop=True,
+                    lhsT=ident[:], rhs=raws[k][:, q // 2, t : t + 2, q % 2 * U : (q % 2 + 1) * U], start=True, stop=True,
                 )
 
         def copy_moved(k, q):
@@ -132,33 +153,32 @@ def tile_tkancell_pa_kernel(
         def layout_calls(k):
             if k >= len(units):
                 return [], []
-            columns = 2 * U * len(units[k])
-            cut = min(1024 if k < 5 else 0, columns)
-            banks = [q for q in range(2 * len(units[k])) if (k, q) in moves]
+            columns = 2 * U * blocks(k)
+            banks = [q for q in range(2 * blocks(k)) if (k, q) in moves]
+            cut = min(banks) * U if banks else columns if k < 5 else 0
             start = cut + len(banks) * U
-            half = (start + columns) // 32 * 16
-            piece = U if k in (0, 4) else 4 * U
+            piece = U if k in (0, 4, 5) else 2 * U
             return (
                 [lambda i=i: lay_out(k, on_vector, i, min(i + piece, cut)) for i in range(0, cut, piece)],
                 [lambda q=q: copy_moved(k, q) for q in banks]
-                + [lambda: lay_out(k, on_scalar, start, half), lambda: lay_out(k, on_scalar, half, columns)],
+                + [lambda i=i: lay_out(k, on_scalar, i, min(i + 2 * U, columns)) for i in range(start, columns, 2 * U)],
             )
 
-        def quantize_weights(k, i):
+        def quantize_weights(k, j):
             if k not in coded:
                 w_codes = w_pool.tile([P, 4, U], U32, align_bytes=64, tag="w_codes")
                 w_scales = w_pool.tile([P, 4, U], U8, align_bytes=64, tag="w_scales")
                 coded[k] = w_codes, w_scales
             w_codes, w_scales = coded[k]
-            passes = slice(2 * i, 2 * i + 2)
+            passes = slice(2 * j, 2 * j + 2)
             nc.vector.quantize_mx(
                 out=w_codes[:, passes].rearrange("p q u -> p (q u)").bitcast(FP8X4),
                 scales=w_scales[:, passes].rearrange("p q u -> p (q u)"),
-                in_=grouped[k][:, 2 * i * U : 2 * (i + 1) * U].rearrange("p c t -> p (c t)"),
+                in_=grouped[k][:, 2 * j * U : 2 * (j + 1) * U].rearrange("p c t -> p (c t)"),
             )
 
         def quantize_calls(k):
-            return [lambda i=i: quantize_weights(k, i) for i in range(len(units[k]))]
+            return [lambda j=j: quantize_weights(k, j) for j in range(blocks(k))] if k < len(units) else []
 
         xT = keep.tile([P, D_HALVES, B, PACK], BF16)
         xT_words = xT[:].bitcast(F32)
@@ -186,27 +206,37 @@ def tile_tkancell_pa_kernel(
                 acc[(L - 1, h, 0)] = acc_pool.tile([P, ROWS], F32, name="acc_%d" % (B_TILES + h))
                 acc[(L - 1, h, 1)] = small.tile([P, ROWS], F32, name="small")
 
-        def multiply(k, halves=(0, 1)):
+        def product(k, step, l, rows, sums, first, final):
             w_codes, w_scales = coded[k]
-            for i, (step, l) in enumerate(units[k]):
-                if l == L - 1 and (l, 0, 0) not in acc:
-                    open_last_accumulators()
-                pieces = [(i, half) for half in halves] if l == L - 1 else [(i, None)]
-                for i, half in pieces:
-                    rows = slice(0, B) if half is None else slice(half * ROWS, (half + 1) * ROWS)
-                    for s in range(2):
-                        for h in range(U_HALVES):
-                            cols = slice(h * P, (h + 1) * P)
-                            out_sums = acc[(l, h)] if half is None else acc[(l, h, half)]
-                            nc.tensor.matmul_mx(
-                                out=out_sums[:],
-                                lhsT=w_codes[:, 2 * i + s, cols].bitcast(FP8X4),
-                                lhsT_scale=w_scales[:, 2 * i + s, cols],
-                                rhs=a_codes[:, step, s, rows].bitcast(FP8X4),
-                                rhs_scale=a_scales[:, step, s, rows],
-                                start=(step == 0 and s == 0),
-                                stop=(step == len(steps) - 1 and s == 1),
-                            )
+            for s in range(2):
+                q = place(k, step, l, s)
+                for h in range(U_HALVES):
+                    cols = slice(h * P, (h + 1) * P)
+                    nc.tensor.matmul_mx(
+                        out=sums[h][:],
+                        lhsT=w_codes[:, q, cols].bitcast(FP8X4),
+                        lhsT_scale=w_scales[:, q, cols],
+                        rhs=a_codes[:, step, s, rows].bitcast(FP8X4),
+                        rhs_scale=a_scales[:, step, s, rows],
+                        start=(first and s == 0),
+                        stop=(final and s == 1),
+                    )
+
+        def unit_of(step, l):
+            return [k for k, (unit_steps, layers) in enumerate(units) if step in unit_steps and l in layers][0]
+
+        def multiply(step, l):
+            sums = [acc[(l, h)] for h in range(U_HALVES)]
+            product(unit_of(step, l), step, l, slice(0, B), sums, step == 0, step == len(steps) - 1)
+
+        def multiply_last(k, halves=(0, 1)):
+            if (L - 1, 0, 0) not in acc:
+                open_last_accumulators()
+            for step in units[k][0]:
+                for half in halves:
+                    sums = [acc[(L - 1, h, half)] for h in range(U_HALVES)]
+                    rows = slice(half * ROWS, (half + 1) * ROWS)
+                    product(k, step, L - 1, rows, sums, step == 0, step == silu)
 
         acts, lefts, distance, square, core, neg_k = {}, {}, {}, {}, {}, {}
 
@@ -336,18 +366,17 @@ def tile_tkancell_pa_kernel(
             )
 
         lstm_sb = keep.tile([P, B_TILES, U], BF16)
-        c_raw = keep.tile([P, 2, PACK, U], BF16)
+        late = {}
         bias_sb = keep.tile([P, U], BF16)
         c_codes = keep.tile([P, 2, U], U32, align_bytes=64)
         c_scales = keep.tile([P, 2, U], U8, align_bytes=64)
         planes = keep.tile([P, 2, PACK, B], BF16)
-        f_codes = keep.tile([P, 2, B], U32, align_bytes=64)
-        f_scales = keep.tile([P, 2, B], U8, align_bytes=64)
 
         def load_projection():
-            nc.sync.dma_start(out=lstm_sb[:], in_=lstm_out.rearrange("(n p) u -> p n u", p=P))
+            c_raw = raw_pool.tile([P, 2 * PACK, U], BF16, name="raw")
+            late["c"] = c_raw
             nc.sync.dma_start(
-                out=c_raw[:].rearrange("p g t u -> p (g t) u"),
+                out=c_raw[:],
                 in_=combine_w.rearrange("(q p) u -> p q u", p=P),
             )
             nc.sync.dma_start(out=bias_sb[:], in_=combine_b.partition_broadcast(P))
@@ -361,17 +390,20 @@ def tile_tkancell_pa_kernel(
                     )
             nc.scalar.copy(out=planes[:, 0, 0:U_HALVES, :], in_=lt[:])
 
-        def quantize_projection():
+        def lay_out_projection():
             c_grouped = grouped_pool.tile([P, 2, U, PACK], BF16, align_bytes=64, name="w_grouped")
+            late["c grouped"] = c_grouped
             for G in range(2):
                 on_scalar(
-                    out=c_grouped[:, G].rearrange("p (c i) t -> p c t i", i=4),
-                    in_=c_raw[:, G].rearrange("p t (c i) -> p c t i", i=4),
+                    out=c_grouped[:, G].rearrange("p (c i) t -> p c t i", i=8),
+                    in_=late["c"][:, G * PACK : (G + 1) * PACK, :].rearrange("p t (c i) -> p c t i", i=8),
                 )
+
+        def quantize_projection():
             nc.vector.quantize_mx(
                 out=c_codes[:].rearrange("p g u -> p (g u)").bitcast(FP8X4),
                 scales=c_scales[:].rearrange("p g u -> p (g u)"),
-                in_=c_grouped[:].rearrange("p g u t -> p (g u t)"),
+                in_=late["c grouped"][:].rearrange("p g u t -> p (g u t)"),
             )
 
         def copy_out(l, engines):
@@ -384,7 +416,7 @@ def tile_tkancell_pa_kernel(
             for h in range(U_HALVES):
                 copiers[h](out=planes[:, 1, U_HALVES + h, rows], in_=acc[(L - 1, h, half)][:])
 
-        f_grouped = {}
+        f_grouped, f_coded = {}, []
 
         def lay_out_combined(G, half, cut):
             if G not in f_grouped:
@@ -394,11 +426,16 @@ def tile_tkancell_pa_kernel(
                 (on_vector, slice(first, first + cut)), (on_scalar, slice(first + cut, first + ROWS))
             ):
                 copy(
-                    out=f_grouped[G][:, rows].rearrange("p (c i) t -> p c t i", i=4),
-                    in_=planes[:, G, :, rows].rearrange("p t (c i) -> p c t i", i=4),
+                    out=f_grouped[G][:, rows].rearrange("p (c i) t -> p c t i", i=8),
+                    in_=planes[:, G, :, rows].rearrange("p t (c i) -> p c t i", i=8),
                 )
 
         def quantize_combined(G, half):
+            if not f_coded:
+                f_codes = w_pool.tile([P, 2, B], U32, align_bytes=64, tag="w_codes")
+                f_scales = w_pool.tile([P, 2, B], U8, align_bytes=64, tag="w_scales")
+                f_coded.extend([f_codes, f_scales])
+            f_codes, f_scales = f_coded
             rows = slice(half * ROWS, (half + 1) * ROWS)
             nc.vector.quantize_mx(
                 out=f_codes[:, G, rows].bitcast(FP8X4),
@@ -414,6 +451,7 @@ def tile_tkancell_pa_kernel(
                     bank = acc_pool.tile([P, U], F32, name="acc_%d" % n)
                     proj.append(bank)
                 rows = slice(n * P, (n + 1) * P)
+                f_codes, f_scales = f_coded
                 nc.tensor.matmul_mx(
                     out=proj[n][:],
                     lhsT=f_codes[:, G, rows].bitcast(FP8X4),
@@ -427,74 +465,70 @@ def tile_tkancell_pa_kernel(
         load_x(0)
         for k in range(4):
             load(k)
-            if k == 0:
+            if k == 1:
                 load_x(1)
-        on_v, on_s = layout_calls(0)
         transpose_x(0, 0)
         transpose_x(0, 1)
-        weave(on_v, [])
         for k in range(3):
-            on_v, on_s = layout_calls(k)
-            if k > 0:
-                weave(on_v, [])
+            weave(layout_calls(k)[0], [])
             if k == 0:
                 weave(scalar_calls(0), [])
                 weave(left_calls(0), [])
+            weave(quantize_calls(k), [])
+            if k == 1:
                 transpose_x(1, 0)
                 transpose_x(1, 1)
-            weave(on_s, [])
-            weave(quantize_calls(k), [])
         open_accumulators()
-        last_shared = units.index([(len(steps) - 1, 0), (len(steps) - 1, 1)])
-        pending = []
+        last = len(units) - 1
+        products = {k: [] for k in range(len(units) + 1)}
+        for step in range(len(steps)):
+            for l in range(L - 1):
+                products[max(turn[step] + 1, unit_of(step, l))].append((step, l))
         for k in range(len(units)):
             if k + 4 < len(units):
                 load(k + 4)
-            if k == 4:
+            if k == 8:
                 load_projection()
             on_v, on_s = layout_calls(k + 3)
+            if k == 4:
+                nc.sync.dma_start(out=lstm_sb[:], in_=lstm_out.rearrange("(n p) u -> p n u", p=P))
             if k == 0:
                 on_v += layout_calls(4)[0]
             if k == 1:
                 on_v = []
-            step, l = units[k][0]
-            fill = [lambda made=made, s=s: quantize_activations(made, s) for made in pending for s in range(2)]
+            step, made = made_at.get(k), made_at.get(k - 1)
+            fill = [lambda s=s: quantize_activations(made, s) for s in range(2)] if made is not None else []
             fill += on_v
-            fill += left_calls(step + 1) if l == 0 else []
+            if step is not None:
+                fill += left_calls(step + 1)
             if k >= 3:
                 fill += quantize_calls(k)
-            pending = []
-            if l == 0:
-                weave(scalar_calls(step + 1), on_s)
-                weave(vector_calls(step), fill)
-                pending = [step]
-            else:
-                weave(on_s, [])
-                weave(fill, [])
+            weave(scalar_calls(step + 1) if step is not None else [], on_s)
+            weave(vector_calls(step) if step is not None else [], fill)
             if k == 1:
                 move(0)
                 move(1)
-            if k == len(units) - 1:
-                multiply(k - 1, [0])
-            elif k > 0:
-                multiply(k - 1)
-            if k == len(units) - 3:
-                quantize_projection()
+            if k > 0 and units[k - 1][1] == (L - 1,) and k - 1 < last - 1:
+                multiply_last(k - 1)
+            for made, l in products[k]:
+                multiply(made, l)
+            if k == last - 3:
+                lay_out_projection()
             if k == 7:
                 transpose_lstm()
-            if k == last_shared + 1:
+            if k == turn[len(steps) - 1] + 1:
                 copy_out(0, [on_scalar, on_scalar])
                 copy_out(1, [on_scalar, on_scalar])
-            if k == len(units) - 1:
-                for half in range(2):
-                    lay_out_combined(0, half, ROWS // 2)
-                for half in range(2):
-                    quantize_combined(0, half)
-        last = len(units) - 1
-        multiply(last, [0])
+        for half in range(2):
+            lay_out_combined(0, half, ROWS // 2)
+        for half in range(2):
+            quantize_combined(0, half)
+        quantize_projection()
+        multiply_last(last - 1, [0])
+        multiply_last(last, [0])
         project(0, range(B_TILES))
-        multiply(last - 1, [1])
-        multiply(last, [1])
+        multiply_last(last - 1, [1])
+        multiply_last(last, [1])
         for half in range(2):
             copy_out_rows(half)
             lay_out_combined(1, half, 176)

import math
from contextlib import ExitStack

import concourse.mybir as mybir
from concourse.masks import make_identity

BF16 = mybir.dt.bfloat16
F32 = mybir.dt.float32
U32 = mybir.dt.uint32
U8 = mybir.dt.uint8
FP8X4 = mybir.dt.float8_e4m3fn_x4
ACT = mybir.ActivationFunctionType
ALU = mybir.AluOpType

P = 128
PACK = 4
K_PASS = P * PACK

B, D, U, L, NB = 512, 1024, 256, 3, 8
FOLD = NB // 2
D_HALVES = D // K_PASS
B_TILES = B // P
U_HALVES = U // P
ROWS = B // 2
WORDS = B * PACK

FLOPS = 2 * B * (D + D * NB) * L * U + 2 * B * (1 + L) * U * U


def weave(main, fill):
    for i in range(max(len(main), len(fill))):
        for calls in (main, fill):
            if i < len(calls):
                calls[i]()


def tile_tkancell_pa_kernel(
    tc, x, lstm_out, kan_base_w, kan_spline_w, combine_w, combine_b, out
):
    nc = tc.nc
    with ExitStack() as ctx:
        keep = ctx.enter_context(tc.tile_pool(name="keep", bufs=1))
        raw_pool = ctx.enter_context(tc.tile_pool(name="raw", bufs=4))
        grouped_pool = ctx.enter_context(tc.tile_pool(name="grouped", bufs=4))
        w_pool = ctx.enter_context(tc.tile_pool(name="w", bufs=4))
        stage = ctx.enter_context(tc.tile_pool(name="stage", bufs=1))
        left_pool = ctx.enter_context(tc.tile_pool(name="left", bufs=2))
        wide = ctx.enter_context(tc.tile_pool(name="wide", bufs=3))
        square_pool = ctx.enter_context(tc.tile_pool(name="squares", bufs=4))
        acc_pool = ctx.enter_context(tc.psum_pool(name="acc", bufs=1))
        small = ctx.enter_context(tc.psum_pool(name="small", bufs=2))

        on_vector = nc.vector.tensor_copy
        on_scalar = nc.scalar.copy
        copiers = [on_vector, on_scalar]

        ident = keep.tile([P, P], BF16)
        make_identity(nc, ident[:])
        ident_words = keep.tile([P, P], F32)
        make_identity(nc, ident_words[:])
        ctx.enter_context(tc.manual_schedule())

        x_halves = []
        x_rows = x.rearrange("(n p) d -> p n d", p=P)

        def load_x(g):
            x_half = square_pool.tile([P, B_TILES, K_PASS], BF16, align_bytes=64, name="sq")
            for n in range(0, B_TILES, 2):
                tiles = slice(n, n + 2)
                nc.sync.dma_start(
                    out=x_half[:, tiles, :], in_=x_rows[:, tiles, g * K_PASS : (g + 1) * K_PASS]
                )
            x_halves.append(x_half)


        steps = [("basis", g, t) for g in range(D_HALVES) for t in range(FOLD)]
        steps.insert(1, ("silu", 0, 0))
        a_codes = keep.tile([P, len(steps), 2, B], U32, align_bytes=64)
        a_scales = keep.tile([P, len(steps), 2, B], U8, align_bytes=64)

        index = {step: i for i, step in enumerate(steps)}
        silu = index[("silu", 0, 0)]
        pairs = [(index[("basis", g, t)], index[("basis", g, t + 1)]) for g in range(D_HALVES) for t in range(0, FOLD, 2)]
        units = [(pair, (l,)) for pair in pairs for l in range(L - 1)]
        units.insert(2, ((silu,), (0, 1)))
        thirds = [(pair, (L - 1,)) for pair in pairs] + [((silu,), (L - 1,))]
        units = units[:8] + thirds[:1] + units[8:] + thirds[1:]
        turn = {step: step if step < 8 else 9 for step in range(len(steps))}
        made_at = {k: step for step, k in turn.items()}

        def blocks(k):
            unit_steps, layers = units[k]
            return 2 if len(unit_steps) == 2 else len(layers)

        base_rows = kan_base_w.rearrange("l (g p t) u -> l g p t u", g=D_HALVES, t=PACK, p=P)
        spline_rows = kan_spline_w.rearrange(
            "l (g p t h i k) u -> l g h i p t (k u)", g=D_HALVES, t=PACK, p=P, h=2, i=FOLD // 2, k=2
        )
        raws, grouped, coded = {}, {}, {}

        def load(k):
            raw = raw_pool.tile([P, 2, PACK, 2 * U], BF16, tag="raw")
            unit_steps, layers = units[k]
            if len(unit_steps) == 2:
                kind, g, t = steps[unit_steps[0]]
                for s in range(2):
                    nc.sync.dma_start(out=raw[:, s], in_=spline_rows[layers[0], g, s, t // 2])
            else:
                for j, l in enumerate(layers):
                    for s in range(2):
                        nc.sync.dma_start(out=raw[:, j, :, s * U : (s + 1) * U], in_=base_rows[l, s])
            raws[k] = raw

        def place(k, step, l, s):
            unit_steps, layers = units[k]
            if len(unit_steps) == 2:
                return 2 * s + unit_steps.index(step)
            return 2 * layers.index(l) + s

        def lay_out(k, copy, first, last):
            if last <= first:
                return
            if k not in grouped:
                grouped[k] = grouped_pool.tile([P, 4 * U, PACK], BF16, align_bytes=64, name="w_grouped")
            j = first // (2 * U)
            columns = slice(first - 2 * j * U, last - 2 * j * U)
            copy(
                out=grouped[k][:, first:last, :].rearrange("p (c i) t -> p c t i", i=8),
                in_=raws[k][:, j, :, columns].rearrange("p t (c i) -> p c t i", i=8),
            )

        moves = [(k, q) for k in range(5, len(units)) for q in range(2 * blocks(k))][2 : 2 + 22]
        moved = {}

        def move(i):
            if i >= len(moves):
                return
            k, q = moves[i]
            moved[i] = small.tile([P, U, PACK], BF16, name="small")
            for t in range(0, PACK, 2):
                nc.tensor.matmul(
                    moved[i][:, :, t : t + 2].rearrange("p c t -> p t c"),
                    lhsT=ident[:], rhs=raws[k][:, q // 2, t : t + 2, q % 2 * U : (q % 2 + 1) * U], start=True, stop=True,
                )

        def copy_moved(k, q):
            i = moves.index((k, q))
            if k not in grouped:
                grouped[k] = grouped_pool.tile([P, 4 * U, PACK], BF16, align_bytes=64, name="w_grouped")
            on_scalar(out=grouped[k][:, q * U : (q + 1) * U, :], in_=moved[i][:])
            move(i + 2)

        def layout_calls(k):
            if k >= len(units):
                return [], []
            columns = 2 * U * blocks(k)
            banks = [q for q in range(2 * blocks(k)) if (k, q) in moves]
            cut = min(banks) * U if banks else columns if k < 5 else 0
            start = cut + len(banks) * U
            piece = U if k in (0, 4, 5) else 2 * U
            return (
                [lambda i=i: lay_out(k, on_vector, i, min(i + piece, cut)) for i in range(0, cut, piece)],
                [lambda q=q: copy_moved(k, q) for q in banks]
                + [lambda i=i: lay_out(k, on_scalar, i, min(i + 2 * U, columns)) for i in range(start, columns, 2 * U)],
            )

        def quantize_weights(k, j):
            if k not in coded:
                w_codes = w_pool.tile([P, 4, U], U32, align_bytes=64, tag="w_codes")
                w_scales = w_pool.tile([P, 4, U], U8, align_bytes=64, tag="w_scales")
                coded[k] = w_codes, w_scales
            w_codes, w_scales = coded[k]
            passes = slice(2 * j, 2 * j + 2)
            nc.vector.quantize_mx(
                out=w_codes[:, passes].rearrange("p q u -> p (q u)").bitcast(FP8X4),
                scales=w_scales[:, passes].rearrange("p q u -> p (q u)"),
                in_=grouped[k][:, 2 * j * U : 2 * (j + 1) * U].rearrange("p c t -> p (c t)"),
            )

        def quantize_calls(k):
            return [lambda j=j: quantize_weights(k, j) for j in range(blocks(k))] if k < len(units) else []

        xT = keep.tile([P, D_HALVES, B, PACK], BF16)
        xT_words = xT[:].bitcast(F32)

        def transpose_x(g, m):
            xt = acc_pool.tile([P, 2, 2, P], F32, name="acc_%d" % (2 * g + m))
            for i in range(2):
                words = x_halves[g][:].bitcast(F32)[:, 2 * m + i, :]
                for u in range(2):
                    nc.tensor.transpose(xt[:, i, u, :], words[:, u : K_PASS // 2 : 2], ident_words[:])
            copiers[m](
                out=xT_words[:, g, 2 * m * P : 2 * (m + 1) * P, :].rearrange("p (i r) u -> p i r u", i=2),
                in_=xt[:].rearrange("p i u r -> p i r u"),
            )

        acc = {}

        def open_accumulators():
            for l in range(L - 1):
                for h in range(U_HALVES):
                    acc[(l, h)] = acc_pool.tile([P, B], F32, name="acc_%d" % (U_HALVES * l + h))

        def open_last_accumulators():
            for h in range(U_HALVES):
                acc[(L - 1, h, 0)] = acc_pool.tile([P, ROWS], F32, name="acc_%d" % (B_TILES + h))
                acc[(L - 1, h, 1)] = small.tile([P, ROWS], F32, name="small")

        def product(k, step, l, rows, sums, first, final):
            w_codes, w_scales = coded[k]
            for s in range(2):
                q = place(k, step, l, s)
                for h in range(U_HALVES):
                    cols = slice(h * P, (h + 1) * P)
                    nc.tensor.matmul_mx(
                        out=sums[h][:],
                        lhsT=w_codes[:, q, cols].bitcast(FP8X4),
                        lhsT_scale=w_scales[:, q, cols],
                        rhs=a_codes[:, step, s, rows].bitcast(FP8X4),
                        rhs_scale=a_scales[:, step, s, rows],
                        start=(first and s == 0),
                        stop=(final and s == 1),
                    )

        def unit_of(step, l):
            return [k for k, (unit_steps, layers) in enumerate(units) if step in unit_steps and l in layers][0]

        def multiply(step, l):
            sums = [acc[(l, h)] for h in range(U_HALVES)]
            product(unit_of(step, l), step, l, slice(0, B), sums, step == 0, step == len(steps) - 1)

        def multiply_last(k, halves=(0, 1)):
            if (L - 1, 0, 0) not in acc:
                open_last_accumulators()
            for step in units[k][0]:
                for half in halves:
                    sums = [acc[(L - 1, h, half)] for h in range(U_HALVES)]
                    rows = slice(half * ROWS, (half + 1) * ROWS)
                    product(k, step, L - 1, rows, sums, step == 0, step == silu)

        acts, lefts, distance, square, core, neg_k = {}, {}, {}, {}, {}, {}

        def features(g):
            return xT[:, g].rearrange("p b t -> p (b t)")

        def scalar_calls(step):
            if step >= len(steps):
                return []
            kind, g, t = steps[step]

            def silu(half):
                if half == 0:
                    acts[step] = square_pool.tile([P, 2, WORDS], BF16, align_bytes=64, name="sq")
                nc.scalar.activation(out=acts[step][:, half, :], in_=features(half), func=ACT.Silu)

            def fold():
                distance[step] = wide.tile([P, WORDS], F32, name="dist")
                half = WORDS // 2
                for span in [slice(0, half), slice(half, WORDS)] if step == 0 else [slice(0, WORDS)]:
                    nc.scalar.activation(
                        out=distance[step][:, span], in_=features(g)[:, span], func=ACT.Abs, scale=2.5, bias=1.5 - t
                    )

            def from_centre():
                nc.scalar.activation(
                    out=distance[step][:], in_=distance[step][:], func=ACT.Abs, bias=-2.0
                )

            def tail_square():
                square[step] = square_pool.tile([P, WORDS], F32, align_bytes=64, name="sq")
                nc.scalar.activation(
                    out=square[step][:], in_=distance[step][:], func=ACT.Square,
                    scale=-math.sqrt(1.0 / 6.0), bias=2.0 * math.sqrt(1.0 / 6.0),
                )

            def from_even_bump():
                core[0] = wide.tile([P, WORDS], F32, name="dist")
                nc.scalar.activation(
                    out=core[0][:], in_=distance[step][:], func=ACT.Abs, scale=-1.0, bias=2.0
                )

            def from_odd_knot():
                nc.scalar.activation(out=core[0][:], in_=core[0][:], func=ACT.Abs, bias=-1.0)

            def core_square(odd):
                core[1 + odd] = square_pool.tile([P, WORDS], F32, align_bytes=64, name="sq")
                nc.scalar.activation(
                    out=core[1 + odd][:], in_=core[0][:], func=ACT.Square,
                    scale=math.sqrt(0.5), bias=(0.0, -0.5)[odd] * math.sqrt(0.5),
                )

            if kind == "silu":
                return [lambda: silu(0), lambda: silu(1)]
            if t == 0:
                return [
                    fold, from_centre, from_even_bump, tail_square, from_odd_knot,
                    lambda: core_square(0), lambda: core_square(1),
                ]
            return [fold, from_centre, tail_square]

        def left_calls(step):
            if step >= len(steps) or steps[step][0] == "silu":
                return []
            kind, g, t = steps[step]

            def compare():
                lefts[step] = left_pool.tile([P, WORDS], BF16, name="left")
                nc.vector.tensor_single_scalar(
                    out=lefts[step][:], in_=features(g), scalar=0.4 * t - 0.6, op=ALU.is_lt
                )

            return [compare]

        def vector_calls(step):
            kind, g, t = steps[step]
            bump = {}

            def cube():
                bump[0] = stage.tile([P, WORDS], BF16, name="bump")
                nc.vector.scalar_tensor_tensor(
                    out=bump[0][:], in0=distance[step][:], scalar=2.0, in1=square[step][:],
                    op0=ALU.subtract, op1=ALU.mult,
                )

            def core_cube():
                nc.vector.scalar_tensor_tensor(
                    out=core[1][:], in0=core[0][:], scalar=2.0, in1=core[1][:], op0=ALU.subtract, op1=ALU.mult,
                )

            def odd_core():
                neg_k[1] = stage.tile([P, WORDS], BF16, name="neg_k1")
                nc.vector.tensor_scalar(
                    out=neg_k[1][:], in0=core[1][:], scalar1=-1.0, scalar2=2.0 / 3.0, op0=ALU.mult, op1=ALU.subtract
                )

            def even_core():
                neg_k[0] = stage.tile([P, WORDS], BF16, name="neg_k0")
                nc.vector.scalar_tensor_tensor(
                    out=neg_k[0][:], in0=core[2][:], scalar=7.0 / 24.0, in1=core[1][:],
                    op0=ALU.subtract, op1=ALU.add,
                )

            def core_or_tail():
                nc.vector.tensor_max(out=bump[0][:], in0=bump[0][:], in1=neg_k[t % 2][:])

            def positive_part():
                nc.vector.tensor_scalar(
                    out=bump[0][:], in0=bump[0][:], scalar1=-1.0, scalar2=0.0, op0=ALU.mult, op1=ALU.max
                )

            def left_basis():
                acts[step] = stage.tile([P, 2, WORDS], BF16, align_bytes=64, name="acts")
                nc.vector.tensor_mul(out=acts[step][:, 0, :], in0=bump[0][:], in1=lefts[step][:])

            def right_basis():
                nc.vector.tensor_sub(out=acts[step][:, 1, :], in0=bump[0][:], in1=acts[step][:, 0, :])

            if kind == "silu":
                return []
            cores = [lambda: (core_cube(), odd_core(), even_core())]
            return [cube] + (cores if t == 0 else []) + [core_or_tail, positive_part, left_basis, right_basis]

        def quantize_activations(step, s):
            nc.vector.quantize_mx(
                out=a_codes[:, step, s, :].bitcast(FP8X4), scales=a_scales[:, step, s, :], in_=acts[step][:, s, :]
            )

        lstm_sb = keep.tile([P, B_TILES, U], BF16)
        late = {}
        bias_sb = keep.tile([P, U], BF16)
        c_codes = keep.tile([P, 2, U], U32, align_bytes=64)
        c_scales = keep.tile([P, 2, U], U8, align_bytes=64)
        planes = keep.tile([P, 2, PACK, B], BF16)

        def load_projection():
            c_raw = raw_pool.tile([P, 2 * PACK, U], BF16, name="raw")
            late["c"] = c_raw
            nc.sync.dma_start(
                out=c_raw[:],
                in_=combine_w.rearrange("(q p) u -> p q u", p=P),
            )
            nc.sync.dma_start(out=bias_sb[:], in_=combine_b.partition_broadcast(P))

        def transpose_lstm():
            lt = small.tile([P, U_HALVES, B], BF16, name="small")
            for n in range(B_TILES):
                for h in range(U_HALVES):
                    nc.tensor.transpose(
                        lt[:, h, n * P : (n + 1) * P], lstm_sb[:, n, h * P : (h + 1) * P], ident[:]
                    )
            nc.scalar.copy(out=planes[:, 0, 0:U_HALVES, :], in_=lt[:])

        def lay_out_projection():
            c_grouped = grouped_pool.tile([P, 2, U, PACK], BF16, align_bytes=64, name="w_grouped")
            late["c grouped"] = c_grouped
            for G in range(2):
                on_scalar(
                    out=c_grouped[:, G].rearrange("p (c i) t -> p c t i", i=8),
                    in_=late["c"][:, G * PACK : (G + 1) * PACK, :].rearrange("p t (c i) -> p c t i", i=8),
                )

        def quantize_projection():
            nc.vector.quantize_mx(
                out=c_codes[:].rearrange("p g u -> p (g u)").bitcast(FP8X4),
                scales=c_scales[:].rearrange("p g u -> p (g u)"),
                in_=late["c grouped"][:].rearrange("p g u t -> p (g u t)"),
            )

        def copy_out(l, engines):
            for h in range(U_HALVES):
                plane = U_HALVES + l * U_HALVES + h
                engines[h](out=planes[:, plane // PACK, plane % PACK, :], in_=acc[(l, h)][:])

        def copy_out_rows(half):
            rows = slice(half * ROWS, (half + 1) * ROWS)
            for h in range(U_HALVES):
                copiers[h](out=planes[:, 1, U_HALVES + h, rows], in_=acc[(L - 1, h, half)][:])

        f_grouped, f_coded = {}, []

        def lay_out_combined(G, half, cut):
            if G not in f_grouped:
                f_grouped[G] = square_pool.tile([P, B, PACK], BF16, align_bytes=64, name="sq")
            first = half * ROWS
            for copy, rows in (
                (on_vector, slice(first, first + cut)), (on_scalar, slice(first + cut, first + ROWS))
            ):
                copy(
                    out=f_grouped[G][:, rows].rearrange("p (c i) t -> p c t i", i=8),
                    in_=planes[:, G, :, rows].rearrange("p t (c i) -> p c t i", i=8),
                )

        def quantize_combined(G, half):
            if not f_coded:
                f_codes = w_pool.tile([P, 2, B], U32, align_bytes=64, tag="w_codes")
                f_scales = w_pool.tile([P, 2, B], U8, align_bytes=64, tag="w_scales")
                f_coded.extend([f_codes, f_scales])
            f_codes, f_scales = f_coded
            rows = slice(half * ROWS, (half + 1) * ROWS)
            nc.vector.quantize_mx(
                out=f_codes[:, G, rows].bitcast(FP8X4),
                scales=f_scales[:, G, rows],
                in_=f_grouped[G][:, rows].rearrange("p b t -> p (b t)"),
            )

        proj = []

        def project(G, tiles):
            for n in tiles:
                if G == 0:
                    bank = acc_pool.tile([P, U], F32, name="acc_%d" % n)
                    proj.append(bank)
                rows = slice(n * P, (n + 1) * P)
                f_codes, f_scales = f_coded
                nc.tensor.matmul_mx(
                    out=proj[n][:],
                    lhsT=f_codes[:, G, rows].bitcast(FP8X4),
                    lhsT_scale=f_scales[:, G, rows],
                    rhs=c_codes[:, G, :].bitcast(FP8X4),
                    rhs_scale=c_scales[:, G, :],
                    start=(G == 0),
                    stop=(G == 1),
                )

        load_x(0)
        for k in range(4):
            load(k)
            if k == 1:
                load_x(1)
        transpose_x(0, 0)
        transpose_x(0, 1)
        for k in range(3):
            weave(layout_calls(k)[0], [])
            if k == 0:
                weave(scalar_calls(0), [])
                weave(left_calls(0), [])
            weave(quantize_calls(k), [])
            if k == 1:
                transpose_x(1, 0)
                transpose_x(1, 1)
        open_accumulators()
        last = len(units) - 1
        products = {k: [] for k in range(len(units) + 1)}
        for step in range(len(steps)):
            for l in range(L - 1):
                products[max(turn[step] + 1, unit_of(step, l))].append((step, l))
        for k in range(len(units)):
            if k + 4 < len(units):
                load(k + 4)
            if k == 8:
                load_projection()
            on_v, on_s = layout_calls(k + 3)
            if k == 4:
                nc.sync.dma_start(out=lstm_sb[:], in_=lstm_out.rearrange("(n p) u -> p n u", p=P))
            if k == 0:
                on_v += layout_calls(4)[0]
            if k == 1:
                on_v = []
            step, made = made_at.get(k), made_at.get(k - 1)
            fill = [lambda s=s: quantize_activations(made, s) for s in range(2)] if made is not None else []
            fill += on_v
            if step is not None:
                fill += left_calls(step + 1)
            if k >= 3:
                fill += quantize_calls(k)
            weave(scalar_calls(step + 1) if step is not None else [], on_s)
            weave(vector_calls(step) if step is not None else [], fill)
            if k == 1:
                move(0)
                move(1)
            if k > 0 and units[k - 1][1] == (L - 1,) and k - 1 < last - 1:
                multiply_last(k - 1)
            for made, l in products[k]:
                multiply(made, l)
            if k == last - 3:
                lay_out_projection()
            if k == 7:
                transpose_lstm()
            if k == turn[len(steps) - 1] + 1:
                copy_out(0, [on_scalar, on_scalar])
                copy_out(1, [on_scalar, on_scalar])
        for half in range(2):
            lay_out_combined(0, half, ROWS // 2)
        for half in range(2):
            quantize_combined(0, half)
        quantize_projection()
        multiply_last(last - 1, [0])
        multiply_last(last, [0])
        project(0, range(B_TILES))
        multiply_last(last - 1, [1])
        multiply_last(last, [1])
        for half in range(2):
            copy_out_rows(half)
            lay_out_combined(1, half, 176)
            quantize_combined(1, half)
        project(1, range(B_TILES))

        result = stage.tile([P, B_TILES, U], F32, align_bytes=64, name="acts")
        out_rows = out.rearrange("(n p) u -> p n u", p=P)
        for n in range(B_TILES):
            nc.vector.tensor_add(out=result[:, n, :], in0=proj[n][:], in1=bias_sb[:])
            nc.sync.dma_start(out=out_rows[:, n, :], in_=result[:, n, :])
